import numpy as np
import ml_dtypes


def mxq(x, axis, fmt="e4m3"):
    dtype, down = {"e4m3": (ml_dtypes.float8_e4m3fn, 7), "e5m2": (ml_dtypes.float8_e5m2, 14)}[fmt]
    v = np.moveaxis(np.asarray(x, np.float32).astype(ml_dtypes.bfloat16).astype(np.float64), axis, -1)
    blocks = v.reshape(v.shape[:-1] + (-1, 32))
    amax = np.abs(blocks).max(-1, keepdims=True)
    byte = np.maximum(np.where(amax > 0, np.frexp(amax)[1] - 1 + 127, 0) - down, 1)
    scale = np.exp2(byte - 127.0)
    codes = (blocks / scale).astype(np.float32).astype(dtype).astype(np.float64)
    return np.moveaxis((codes * scale).reshape(v.shape), -1, axis)


WIDE = False


def mx_kscale(k):
    if not WIDE:
        return np.ones(k)
    levels = np.array([10, -10, 5, -5, 0])
    a = np.random.permutation(np.resize(levels, k // 512 * 4)).reshape(k // 512, 4)
    idx = np.arange(k)
    return np.exp2(a[idx // 512, idx % 128 // 32])


BF16 = ml_dtypes.bfloat16


def bf(x):
    return np.asarray(x, np.float32).astype(BF16)


def f64(x):
    return np.asarray(x).astype(np.float64)


B, J, C, K, H, M = 16, 256, 512, 2, 8, 256
DH = C // H
S_G2A, S_A2G = 0.5, 0.8


def setup_inputs():
    s = mx_kscale(C)
    return {'attn_o': bf(np.random.standard_normal((B, H, J, DH)) * 0.6 * s.reshape(H, 1, DH)),
            'xg1': bf(np.random.standard_normal((B, J, C)) * 0.7 * s),
            'x': bf(np.random.standard_normal((B, J, C))),
            'adj': bf(np.random.uniform(size=(K, J, J)) / np.sqrt(K * J)),
            'proj_w': bf(np.random.standard_normal((C, C)) / np.sqrt(C) / s),
            'proj_b': bf(0.1 * np.random.standard_normal(C)),
            'gcn2_w': bf(np.random.standard_normal((K * C, C)) * 1.5 / np.sqrt(C) / s),
            'gcn2_b': bf(np.random.standard_normal(K * C) * 0.6 / np.sqrt(J))}


def reference(attn_o, xg1, x, adj, proj_w, proj_b, gcn2_w, gcn2_b):
    o = f64(attn_o)
    g1 = f64(xg1)
    attn2gcn = o.transpose(0, 2, 1, 3).reshape(B, J, C)
    fh = (g1 * S_G2A).reshape(B, J, H, DH).transpose(0, 2, 1, 3)
    v = (o + fh).transpose(0, 2, 1, 3).reshape(B, J, C)
    xa = (mxq(v, 2, 'e4m3') @ mxq(f64(proj_w), 1, 'e4m3').T) + f64(proj_b)
    u = g1 + attn2gcn * S_A2G
    y = (mxq(u, 2, 'e4m3') @ mxq(f64(gcn2_w), 1, 'e4m3').T) + f64(gcn2_b)
    yk = y.reshape(B, J, K, C).transpose(0, 2, 1, 3).reshape(B, K * J, C)
    a = f64(adj).reshape(K * J, J)
    xg2 = mxq(a, 0, 'e4m3').T @ mxq(yk, 1, 'e4m3')
    return f64(x) + xg2 + xa

@@ -1,0 +1,313 @@
+from contextlib import ExitStack
+
+import concourse.mybir as mybir
+from concourse.masks import make_identity
+
+FP8X4 = mybir.dt.float8_e4m3fn_x4
+BF16 = mybir.dt.bfloat16
+F32 = mybir.dt.float32
+U32 = mybir.dt.uint32
+U8 = mybir.dt.uint8
+ADD = mybir.AluOpType.add
+MULT = mybir.AluOpType.mult
+COPY = mybir.ActivationFunctionType.Copy
+
+B, J, C, K, H = 16, 256, 512, 2, 8
+DH = C // H
+P = 128
+PACK = 4
+HALF = P // 2
+TILES = J // P
+S_G2A, S_A2G = 0.5, 0.8
+INV_A2G = 1.25
+assert INV_A2G * S_A2G == 1.0
+
+FLOPS = 2 * B * J * C * (C + K * C) + 2 * B * J * (K * J) * C
+
+
+def tile_block_pb_t_kernel(tc, attn_o, xg1, x, adj, proj_w, proj_b, gcn2_w, gcn2_b, out):
+    nc = tc.nc
+    with ExitStack() as stack:
+        consts = stack.enter_context(tc.tile_pool(name="consts", bufs=1))
+        staging = stack.enter_context(tc.tile_pool(name="staging", bufs=1))
+        resident = stack.enter_context(tc.tile_pool(name="resident", bufs=B))
+        ring = stack.enter_context(tc.tile_pool(name="ring", bufs=6))
+        work = stack.enter_context(tc.tile_pool(name="work", bufs=2))
+        psum_front = stack.enter_context(tc.psum_pool(name="psum_front", bufs=3))
+        psum_y = stack.enter_context(tc.psum_pool(name="psum_y", bufs=3))
+        psum_f = stack.enter_context(tc.psum_pool(name="psum_f", bufs=2))
+
+        ident_f32 = consts.tile([P, P], F32, name="ident_f32")
+        make_identity(nc, ident_f32[:])
+        ident_bf = consts.tile([P, P], BF16, name="ident_bf")
+        make_identity(nc, ident_bf[:])
+        ones = consts.tile([P, P], BF16, name="ones")
+        nc.vector.memset(ones[:], 1.0)
+        combine = consts.tile([P, HALF], BF16, name="combine")
+        pairs = ident_bf[:].rearrange("p (i s) -> p s i", s=2)
+        nc.vector.scalar_tensor_tensor(
+            out=combine[:], in0=pairs[:, 1], scalar=INV_A2G, in1=pairs[:, 0], op0=MULT, op1=ADD
+        )
+
+        bias_row = consts.tile([P, K * C + C], BF16, name="bias_row")
+        nc.vector.memset(bias_row[:], 0.0)
+        nc.scalar.dma_start(out=bias_row[0:1, 0 : K * C], in_=gcn2_b.unsqueeze(0))
+        nc.scalar.dma_start(out=bias_row[0:1, K * C : K * C + C], in_=proj_b.unsqueeze(0))
+
+        wg_raw = staging.tile([P, PACK * K * C], BF16, name="wg_raw")
+        wg_rows = gcn2_w.rearrange("(k cc p) c -> cc p k c", k=K, cc=PACK)
+
+        def load_gcn_weight_chunk(cc):
+            nc.sync.dma_start(
+                out=wg_raw[:, cc * K * C : (cc + 1) * K * C].rearrange("p (k c) -> p k c", k=K), in_=wg_rows[cc]
+            )
+
+        stacked = {}
+
+        def load_streams(b):
+            ag = resident.tile([P, PACK * C], BF16, tag="ag", name="ag")
+            heads = attn_o[b].rearrange("h (mh i wh) d -> mh wh i h d", mh=2, wh=2)
+            for mh in range(2):
+                for wh in range(2):
+                    e = 2 * mh + wh
+                    nc.sync.dma_start(
+                        out=ag[0:P:2, e * C : (e + 1) * C].rearrange("i (h d) -> i h d", h=H), in_=heads[mh, wh]
+                    )
+            nc.sync.dma_start(
+                out=ag[1:P:2, :].rearrange("i (mh r) -> i mh r", mh=2),
+                in_=xg1[b].rearrange("(mh i wh) c -> i mh (wh c)", mh=2, wh=2),
+            )
+            stacked[b] = ag
+
+        residual_in = {}
+
+        def load_residual(b):
+            x_sb = ring.tile([P, TILES * C], BF16, tag="x", name="x_sb")
+            nc.sync.dma_start(out=x_sb[:], in_=x[b].rearrange("(m wh) c -> m (wh c)", wh=TILES))
+            residual_in[b] = x_sb
+
+        load_gcn_weight_chunk(0)
+        load_streams(0)
+        for cc in range(1, PACK):
+            load_gcn_weight_chunk(cc)
+        adj_raw = staging.tile([P, K * TILES * J], BF16, name="adj_raw")
+        nc.sync.dma_start(
+            out=adj_raw[:].rearrange("p (k r) -> p k r", k=K), in_=adj.rearrange("k (m jh) w -> m k (jh w)", jh=TILES)
+        )
+        wp_raw = staging.tile([P, PACK * C], BF16, name="wp_raw")
+        nc.sync.dma_start(
+            out=wp_raw[:].rearrange("p (ot c) -> p ot c", ot=PACK), in_=proj_w.rearrange("(ot p) c -> p ot c", p=P)
+        )
+        load_streams(1)
+
+        gb_sb = consts.tile([P, C * K], F32, name="gb_sb")
+        for hf in range(2):
+            g_ps = psum_front.tile([P, K, C // 2], F32, tag="front", name="g_ps")
+            for k in range(K):
+                col = k * C + hf * (C // 2)
+                nc.tensor.matmul(g_ps[:, k, :], lhsT=ones[:], rhs=bias_row[:, col : col + C // 2], start=True, stop=True)
+            nc.vector.tensor_copy(
+                out=gb_sb[:, hf * C : (hf + 1) * C].rearrange("p (c k) -> p c k", k=K),
+                in_=g_ps[:].rearrange("p k c -> p c k"),
+            )
+        pb_sb = consts.tile([P, C], F32, name="pb_sb")
+        p_ps = psum_front.tile([P, C], F32, tag="front", name="p_ps")
+        nc.tensor.matmul(p_ps[:], lhsT=ones[:], rhs=bias_row[:, K * C : K * C + C], start=True, stop=True)
+        nc.vector.tensor_copy(out=pb_sb[:], in_=p_ps[:])
+
+        residual = {}
+
+        def add_proj_bias(b):
+            xb = resident.tile([P, TILES * C], F32, tag="xb", name="xb")
+            for wh in range(TILES):
+                cols = slice(wh * C, (wh + 1) * C)
+                nc.gpsimd.tensor_tensor(out=xb[:, cols], in0=residual_in[b][:, cols], in1=pb_sb[:], op=ADD)
+            residual[b] = xb
+
+        for b in range(B):
+            if b + 2 < B:
+                load_streams(b + 2)
+            load_residual(b)
+            add_proj_bias(b)
+
+        wg_grp = staging.tile([P, K * C * PACK], BF16, name="wg_grp", align_bytes=64)
+        wg_codes = consts.tile([P, K * C], U32, name="wg_codes", align_bytes=64)
+        wg_scales = consts.tile([P, K * C], U8, name="wg_scales", align_bytes=64)
+        for cc in range(PACK):
+            w_ps = psum_y.tile([P, PACK, K, P], BF16, tag="y", name="w_ps")
+            for t in range(PACK):
+                for k in range(K):
+                    col = (cc * K + k) * C + t * P
+                    nc.tensor.transpose(w_ps[:, t, k, :], wg_raw[:, col : col + P], ident_bf[:])
+            chunk = wg_grp[:, cc * K * C : (cc + 1) * K * C]
+            grouped = chunk.rearrange("p (c k t) -> p c k t", k=K, t=PACK)
+            if cc % 2 == 0:
+                nc.scalar.copy(out=grouped, in_=w_ps[:].rearrange("p t k c -> p c k t"))
+            else:
+                nc.vector.tensor_copy(out=grouped, in_=w_ps[:].rearrange("p t k c -> p c k t"))
+            cols = slice(cc * K * P, (cc + 1) * K * P)
+            nc.vector.quantize_mx(out=wg_codes[:, cols].bitcast(FP8X4), scales=wg_scales[:, cols], in_=chunk)
+
+        wp_grp = staging.tile([P, C * PACK], BF16, name="wp_grp", align_bytes=64)
+        wp_codes = consts.tile([P, C], U32, name="wp_codes", align_bytes=64)
+        wp_scales = consts.tile([P, C], U8, name="wp_scales", align_bytes=64)
+        wp_words = wp_raw[:].bitcast(F32)
+        for hf in range(2):
+            w_ps = psum_front.tile([P, 2, 2, P], F32, tag="front", name="wp_ps")
+            for u in range(2):
+                for o2 in range(2):
+                    col = (hf * 2 + o2) * (C // 2) + u * P
+                    nc.tensor.transpose(w_ps[:, u, o2, :], wp_words[:, col : col + P], ident_f32[:])
+            nc.scalar.copy(
+                out=wp_grp[:].bitcast(F32)[:, hf * C : (hf + 1) * C].rearrange("q (o u) -> q o u", u=2),
+                in_=w_ps[:].rearrange("q u o2 o -> q (o2 o) u"),
+            )
+        nc.vector.quantize_mx(out=wp_codes[:].bitcast(FP8X4), scales=wp_scales[:], in_=wp_grp[:])
+
+        adj_grp = staging.tile([P, J * PACK], BF16, name="adj_grp", align_bytes=64)
+        adj_codes = consts.tile([P, J], U32, name="adj_codes", align_bytes=64)
+        adj_scales = consts.tile([P, J], U8, name="adj_scales", align_bytes=64)
+        adj_view = adj_raw[:].rearrange("p (k jh mw wh) -> p wh mw jh k", k=K, jh=TILES, wh=TILES)
+        for wh in range(TILES):
+            nc.vector.tensor_copy(
+                out=adj_grp[:, wh * C : (wh + 1) * C].rearrange("p (mw jh k) -> p mw jh k", jh=TILES, k=K),
+                in_=adj_view[:, wh],
+            )
+        nc.vector.quantize_mx(out=adj_codes[:].bitcast(FP8X4), scales=adj_scales[:], in_=adj_grp[:])
+
+        fused = {}
+
+        def transpose_and_combine(b):
+            ag = stacked[b]
+            ag_words = ag[:].bitcast(F32)
+            a_sb = work.tile([P, J * PACK], BF16, tag="a_sb", name="a_sb")
+            g_sb = work.tile([P, J * PACK], BF16, tag="g_sb", name="g_sb")
+            h_sb = work.tile([P, J * PACK], BF16, tag="h_sb", name="h_sb")
+            vu_grp = work.tile([P, 2 * J * PACK], BF16, tag="vu_grp", name="vu_grp", align_bytes=64)
+            a_words = a_sb[:].bitcast(F32).rearrange("q (wh mh i u) -> q wh mh i u", wh=TILES, mh=2, u=2)
+            g_words = g_sb[:].bitcast(F32).rearrange("q (wh mh i u) -> q wh mh i u", wh=TILES, mh=2, u=2)
+            for wh in range(TILES):
+                t_ps = psum_front.tile([P, 2, 2, P], F32, tag="front", name="t_ps")
+                for u in range(2):
+                    for mh in range(2):
+                        col = (2 * mh + wh) * (C // 2) + u * P
+                        nc.tensor.transpose(t_ps[:, u, mh, :], ag_words[:, col : col + P], ident_f32[:])
+                split = t_ps[:].rearrange("q u mh (i s) -> q s mh i u", s=2)
+                nc.scalar.copy(out=a_words[:, wh], in_=split[:, 0])
+                nc.scalar.copy(out=g_words[:, wh], in_=split[:, 1])
+            for jh in range(TILES):
+                u_ps = psum_front.tile([P, PACK, P], F32, tag="front", name="u_ps")
+                for t in range(PACK):
+                    for mh in range(2):
+                        col = (2 * mh + jh) * C + t * P
+                        nc.tensor.matmul(
+                            u_ps[:, t, mh * HALF : (mh + 1) * HALF],
+                            lhsT=ag[:, col : col + P],
+                            rhs=combine[:],
+                            start=True,
+                            stop=True,
+                        )
+                first = (TILES + jh) * P * PACK
+                nc.scalar.activation(
+                    out=vu_grp[:, first : first + P * PACK].rearrange("p (m t) -> p m t", t=PACK),
+                    in_=u_ps[:].rearrange("p t m -> p m t"),
+                    func=COPY,
+                    scale=S_A2G,
+                )
+            nc.scalar.activation(out=h_sb[:], in_=g_sb[:], func=COPY, scale=S_G2A)
+            fused[b] = (a_sb, h_sb, vu_grp)
+
+        operands = {}
+
+        def quantise_streams(b):
+            a_sb, h_sb, vu_grp = fused[b]
+            nc.vector.tensor_tensor(out=vu_grp[:, 0 : J * PACK], in0=a_sb[:], in1=h_sb[:], op=ADD)
+            vu_codes = work.tile([P, 2 * J], U32, tag="vu_codes", name="vu_codes", align_bytes=64)
+            vu_scales = work.tile([P, 2 * J], U8, tag="vu_scales", name="vu_scales", align_bytes=64)
+            nc.vector.quantize_mx(out=vu_codes[:].bitcast(FP8X4), scales=vu_scales[:], in_=vu_grp[:])
+            operands[b] = (vu_codes, vu_scales)
+
+        graph = {}
+
+        def graph_linear(b):
+            vu_codes, vu_scales = operands[b]
+            y_grp = work.tile([P, C * PACK], BF16, tag="y_grp", name="y_grp", align_bytes=64)
+            for cc in range(PACK):
+                y_ps = psum_y.tile([P, TILES, K * P], F32, tag="y", name="y_ps")
+                w_cols = slice(cc * K * P, (cc + 1) * K * P)
+                for jh in range(TILES):
+                    u_cols = slice((TILES + jh) * P, (TILES + jh + 1) * P)
+                    nc.tensor.matmul_mx(
+                        out=y_ps[:, jh, :],
+                        lhsT=vu_codes[:, u_cols].bitcast(FP8X4),
+                        lhsT_scale=vu_scales[:, u_cols],
+                        rhs=wg_codes[:, w_cols].bitcast(FP8X4),
+                        rhs_scale=wg_scales[:, w_cols],
+                        start=True,
+                        stop=True,
+                    )
+                nc.vector.tensor_tensor(
+                    out=y_grp[:, cc * C : (cc + 1) * C].rearrange("p (c jh k) -> p c jh k", jh=TILES, k=K),
+                    in0=y_ps[:].rearrange("p jh (c k) -> p c jh k", k=K),
+                    in1=gb_sb[:, w_cols].rearrange("p (c k) -> p c k", k=K).unsqueeze(2).to_broadcast([P, P, TILES, K]),
+                    op=ADD,
+                )
+            graph[b] = y_grp
+
+        sums = {}
+
+        def open_output_sums(b):
+            vu_codes, vu_scales = operands[b]
+            banks = []
+            for wh in range(TILES):
+                f_ps = psum_f.tile([P, C], F32, tag="f", name="f_ps")
+                v_cols = slice(wh * P, (wh + 1) * P)
+                nc.tensor.matmul_mx(
+                    out=f_ps[:],
+                    lhsT=vu_codes[:, v_cols].bitcast(FP8X4),
+                    lhsT_scale=vu_scales[:, v_cols],
+                    rhs=wp_codes[:].bitcast(FP8X4),
+                    rhs_scale=wp_scales[:],
+                    start=True,
+                    stop=False,
+                )
+                banks.append(f_ps)
+            sums[b] = banks
+
+        def quantise_graph(b):
+            y_codes = work.tile([P, C], U32, tag="y_codes", name="y_codes", align_bytes=64)
+            y_scales = work.tile([P, C], U8, tag="y_scales", name="y_scales", align_bytes=64)
+            nc.vector.quantize_mx(out=y_codes[:].bitcast(FP8X4), scales=y_scales[:], in_=graph[b][:])
+            graph[b] = (y_codes, y_scales)
+
+        def aggregate_and_store(b):
+            y_codes, y_scales = graph[b]
+            xb = residual[b]
+            for wh in range(TILES):
+                w_cols = slice(wh * P, (wh + 1) * P)
+                nc.tensor.matmul_mx(
+                    out=sums[b][wh][:],
+                    lhsT=adj_codes[:, w_cols].bitcast(FP8X4),
+                    lhsT_scale=adj_scales[:, w_cols],
+                    rhs=y_codes[:].bitcast(FP8X4),
+                    rhs_scale=y_scales[:],
+                    start=False,
+                    stop=True,
+                )
+            for wh in range(TILES):
+                cols = slice(wh * C, (wh + 1) * C)
+                nc.vector.tensor_tensor(out=xb[:, cols], in0=sums[b][wh][:], in1=xb[:, cols], op=ADD)
+            nc.sync.dma_start(out=out[b].rearrange("(m wh) c -> m (wh c)", wh=TILES), in_=xb[:])
+
+        transpose_and_combine(0)
+        quantise_streams(0)
+        transpose_and_combine(1)
+        for b in range(B):
+            graph_linear(b)
+            open_output_sums(b)
+            if b + 2 < B:
+                transpose_and_combine(b + 2)
+            quantise_graph(b)
+            if b + 1 < B:
+                quantise_streams(b + 1)
+            aggregate_and_store(b)

@@ -11,16 +11,17 @@ U8 = mybir.dt.uint8
 ADD = mybir.AluOpType.add
 MULT = mybir.AluOpType.mult
 COPY = mybir.ActivationFunctionType.Copy
+IDENTITY = mybir.ActivationFunctionType.Identity
 
 B, J, C, K, H = 16, 256, 512, 2, 8
 DH = C // H
 P = 128
 PACK = 4
-HALF = P // 2
-TILES = J // P
-S_G2A, S_A2G = 0.5, 0.8
-INV_A2G = 1.25
-assert INV_A2G * S_A2G == 1.0
+Q = J // P
+AHEAD = 6
+CHUNK = K * P
+DIRECT = (3,)
+TURNED = tuple(cc for cc in range(PACK) if cc not in DIRECT)
 
 FLOPS = 2 * B * J * C * (C + K * C) + 2 * B * J * (K * J) * C
 
@@ -30,9 +31,9 @@ def tile_block_pb_t_kernel(tc, attn_o, xg1, x, adj, proj_w, proj_b, gcn2_w, gcn2
     with ExitStack() as stack:
         consts = stack.enter_context(tc.tile_pool(name="consts", bufs=1))
         staging = stack.enter_context(tc.tile_pool(name="staging", bufs=1))
-        resident = stack.enter_context(tc.tile_pool(name="resident", bufs=B))
-        ring = stack.enter_context(tc.tile_pool(name="ring", bufs=6))
-        work = stack.enter_context(tc.tile_pool(name="work", bufs=2))
+        loads = stack.enter_context(tc.tile_pool(name="loads", bufs=8))
+        sums = stack.enter_context(tc.tile_pool(name="sums", bufs=8))
+        work = stack.enter_context(tc.tile_pool(name="work", bufs=3))
         psum_front = stack.enter_context(tc.psum_pool(name="psum_front", bufs=3))
         psum_y = stack.enter_context(tc.psum_pool(name="psum_y", bufs=3))
         psum_f = stack.enter_context(tc.psum_pool(name="psum_f", bufs=2))
@@ -41,13 +42,10 @@ def tile_block_pb_t_kernel(tc, attn_o, xg1, x, adj, proj_w, proj_b, gcn2_w, gcn2
         make_identity(nc, ident_f32[:])
         ident_bf = consts.tile([P, P], BF16, name="ident_bf")
         make_identity(nc, ident_bf[:])
+        ident_25 = consts.tile([P, P], BF16, name="ident_25")
+        nc.vector.tensor_scalar(out=ident_25[:], in0=ident_bf[:], scalar1=2.5, scalar2=None, op0=MULT)
         ones = consts.tile([P, P], BF16, name="ones")
         nc.vector.memset(ones[:], 1.0)
-        combine = consts.tile([P, HALF], BF16, name="combine")
-        pairs = ident_bf[:].rearrange("p (i s) -> p s i", s=2)
-        nc.vector.scalar_tensor_tensor(
-            out=combine[:], in0=pairs[:, 1], scalar=INV_A2G, in1=pairs[:, 0], op0=MULT, op1=ADD
-        )
 
         bias_row = consts.tile([P, K * C + C], BF16, name="bias_row")
         nc.vector.memset(bias_row[:], 0.0)
@@ -62,54 +60,62 @@ def tile_block_pb_t_kernel(tc, attn_o, xg1, x, adj, proj_w, proj_b, gcn2_w, gcn2
                 out=wg_raw[:, cc * K * C : (cc + 1) * K * C].rearrange("p (k c) -> p k c", k=K), in_=wg_rows[cc]
             )
 
-        stacked = {}
+        streams = {}
 
         def load_streams(b):
-            ag = resident.tile([P, PACK * C], BF16, tag="ag", name="ag")
-            heads = attn_o[b].rearrange("h (mh i wh) d -> mh wh i h d", mh=2, wh=2)
-            for mh in range(2):
-                for wh in range(2):
-                    e = 2 * mh + wh
-                    nc.sync.dma_start(
-                        out=ag[0:P:2, e * C : (e + 1) * C].rearrange("i (h d) -> i h d", h=H), in_=heads[mh, wh]
-                    )
+            a_raw = loads.tile([P, Q * C], BF16, tag="a_raw", name="a_raw")
             nc.sync.dma_start(
-                out=ag[1:P:2, :].rearrange("i (mh r) -> i mh r", mh=2),
-                in_=xg1[b].rearrange("(mh i wh) c -> i mh (wh c)", mh=2, wh=2),
+                out=a_raw[:].rearrange("p (h r) -> p h r", h=H), in_=attn_o[b].rearrange("h (p q) d -> p h (q d)", q=Q)
             )
-            stacked[b] = ag
+            g_raw = loads.tile([P, Q * C], BF16, tag="g_raw", name="g_raw")
+            nc.sync.dma_start(out=g_raw[:], in_=xg1[b].rearrange("(p q) c -> p (q c)", q=Q))
+            streams[b] = (a_raw, g_raw)
 
         residual_in = {}
 
         def load_residual(b):
-            x_sb = ring.tile([P, TILES * C], BF16, tag="x", name="x_sb")
-            nc.sync.dma_start(out=x_sb[:], in_=x[b].rearrange("(m wh) c -> m (wh c)", wh=TILES))
+            x_sb = loads.tile([P, Q * C], BF16, tag="x_sb", name="x_sb")
+            nc.sync.dma_start(out=x_sb[:], in_=x[b].rearrange("(p q) c -> p (q c)", q=Q))
             residual_in[b] = x_sb
 
         load_gcn_weight_chunk(0)
         load_streams(0)
         for cc in range(1, PACK):
             load_gcn_weight_chunk(cc)
-        adj_raw = staging.tile([P, K * TILES * J], BF16, name="adj_raw")
+        load_streams(1)
+        adj_raw = staging.tile([P, K * Q * J], BF16, name="adj_raw")
         nc.sync.dma_start(
-            out=adj_raw[:].rearrange("p (k r) -> p k r", k=K), in_=adj.rearrange("k (m jh) w -> m k (jh w)", jh=TILES)
+            out=adj_raw[:].rearrange("p (k r) -> p k r", k=K), in_=adj.rearrange("k (m jh) w -> m k (jh w)", jh=Q)
         )
         wp_raw = staging.tile([P, PACK * C], BF16, name="wp_raw")
         nc.sync.dma_start(
             out=wp_raw[:].rearrange("p (ot c) -> p ot c", ot=PACK), in_=proj_w.rearrange("(ot p) c -> p ot c", p=P)
         )
-        load_streams(1)
+        load_streams(2)
+        for b in range(AHEAD):
+            load_residual(b)
+            if b + 3 < AHEAD:
+                load_streams(b + 3)
 
-        gb_sb = consts.tile([P, C * K], F32, name="gb_sb")
-        for hf in range(2):
-            g_ps = psum_front.tile([P, K, C // 2], F32, tag="front", name="g_ps")
-            for k in range(K):
-                col = k * C + hf * (C // 2)
-                nc.tensor.matmul(g_ps[:, k, :], lhsT=ones[:], rhs=bias_row[:, col : col + C // 2], start=True, stop=True)
-            nc.vector.tensor_copy(
-                out=gb_sb[:, hf * C : (hf + 1) * C].rearrange("p (c k) -> p c k", k=K),
-                in_=g_ps[:].rearrange("p k c -> p c k"),
+        bias_pairs = consts.tile([P, K * C], BF16, name="bias_pairs")
+        nc.vector.tensor_copy(
+            out=bias_pairs[:].rearrange("p (c k) -> p c k", k=K),
+            in_=bias_row[:, 0 : K * C].rearrange("p (k c) -> p c k", k=K),
+        )
+        bias_col = consts.tile([P, K * PACK], F32, name="bias_col")
+        c_ps = psum_front.tile([P, K * PACK, 2], F32, tag="front", name="c_ps")
+        for ob in range(K * PACK):
+            nc.tensor.matmul(
+                c_ps[:, ob, :], lhsT=bias_pairs[:, ob * P : (ob + 1) * P], rhs=ones[:, 0:2], start=True, stop=True
             )
+        nc.vector.tensor_copy(out=bias_col[:].unsqueeze(2), in_=c_ps[:, :, 0:1])
+        gb_sb = consts.tile([P, len(DIRECT) * CHUNK], F32, name="gb_sb")
+        for n, cc in enumerate(DIRECT):
+            g_ps = psum_front.tile([P, CHUNK], F32, tag="front", name="g_ps")
+            nc.tensor.matmul(
+                g_ps[:], lhsT=ones[:], rhs=bias_pairs[:, cc * CHUNK : (cc + 1) * CHUNK], start=True, stop=True
+            )
+            nc.vector.tensor_copy(out=gb_sb[:, n * CHUNK : (n + 1) * CHUNK], in_=g_ps[:])
         pb_sb = consts.tile([P, C], F32, name="pb_sb")
         p_ps = psum_front.tile([P, C], F32, tag="front", name="p_ps")
         nc.tensor.matmul(p_ps[:], lhsT=ones[:], rhs=bias_row[:, K * C : K * C + C], start=True, stop=True)
@@ -118,18 +124,196 @@ def tile_block_pb_t_kernel(tc, attn_o, xg1, x, adj, proj_w, proj_b, gcn2_w, gcn2
         residual = {}
 
         def add_proj_bias(b):
-            xb = resident.tile([P, TILES * C], F32, tag="xb", name="xb")
-            for wh in range(TILES):
-                cols = slice(wh * C, (wh + 1) * C)
-                nc.gpsimd.tensor_tensor(out=xb[:, cols], in0=residual_in[b][:, cols], in1=pb_sb[:], op=ADD)
+            xb = sums.tile([P, Q * C], F32, tag="xb", name="xb")
+            nc.gpsimd.tensor_tensor(out=xb[:, 0:C], in0=residual_in[b][:, 0:C], in1=pb_sb[:], op=ADD)
+            nc.vector.tensor_tensor(out=xb[:, C : 2 * C], in0=residual_in[b][:, C : 2 * C], in1=pb_sb[:], op=ADD)
             residual[b] = xb
 
-        for b in range(B):
-            if b + 2 < B:
-                load_streams(b + 2)
-            load_residual(b)
-            add_proj_bias(b)
+        natural = {}
 
+        def fuse_streams(b):
+            a_raw, g_raw = streams[b]
+            a2 = work.tile([P, Q * C], BF16, tag="a2", name="a2")
+            nc.vector.tensor_scalar(
+                out=a2[:].rearrange("p (q h d) -> p q h d", q=Q, h=H),
+                in0=a_raw[:].rearrange("p (h q d) -> p q h d", h=H, q=Q),
+                scalar1=2.0,
+                scalar2=None,
+                op0=MULT,
+            )
+            u_nat = work.tile([P, C], BF16, tag="u_nat", name="u_nat")
+            nc.vector.scalar_tensor_tensor(
+                out=u_nat[:], in0=a2[:, C : 2 * C], scalar=0.4, in1=g_raw[:, C : 2 * C], op0=MULT, op1=ADD
+            )
+            v_nat = work.tile([P, Q * C], BF16, tag="v_nat", name="v_nat")
+            nc.vector.tensor_tensor(out=v_nat[:], in0=a2[:], in1=g_raw[:], op=ADD)
+            natural[b] = (a2, g_raw, u_nat, v_nat)
+
+        grouped = {}
+
+        def turn_streams(b):
+            a2, g_raw, u_nat, v_nat = natural[b]
+            vu_grp = work.tile([P, 2 * J * PACK], BF16, tag="vu_grp", name="vu_grp", align_bytes=64)
+            v_words = v_nat[:].bitcast(F32)
+            v_ps = psum_front.tile([P, Q, 2, P], F32, tag="front", name="v_ps")
+            for q in range(Q):
+                for w in range(2):
+                    col = (2 * q + w) * P
+                    nc.tensor.transpose(v_ps[:, q, w, :], v_words[:, col : col + P], ident_f32[:])
+            nc.scalar.copy(
+                out=vu_grp[:].bitcast(F32)[:, 0 : J * 2].rearrange("p (q m w) -> p q m w", q=Q, w=2),
+                in_=v_ps[:].rearrange("p q w m -> p q m w"),
+            )
+            u_ps = psum_front.tile([P, PACK, P], BF16, tag="front", name="u_ps")
+            for t in range(PACK):
+                nc.tensor.transpose(u_ps[:, t, :], u_nat[:, t * P : (t + 1) * P], ident_bf[:])
+            first = (J + P) * PACK
+            nc.scalar.copy(
+                out=vu_grp[:, first : first + P * PACK].rearrange("p (m t) -> p m t", t=PACK),
+                in_=u_ps[:].rearrange("p t m -> p m t"),
+            )
+            s_ps = psum_front.tile([P, PACK, P], F32, tag="front", name="s_ps")
+            for t in range(PACK):
+                cols = slice(t * P, (t + 1) * P)
+                nc.tensor.matmul(s_ps[:, t, :], lhsT=a2[:, cols], rhs=ident_bf[:], start=True, stop=False)
+                nc.tensor.matmul(s_ps[:, t, :], lhsT=g_raw[:, cols], rhs=ident_25[:], start=False, stop=True)
+            first = J * PACK
+            nc.scalar.activation(
+                out=vu_grp[:, first : first + P * PACK].rearrange("p (m t) -> p m t", t=PACK),
+                in_=s_ps[:].rearrange("p t m -> p m t"),
+                func=COPY,
+                scale=0.4,
+            )
+            grouped[b] = vu_grp
+
+        operands = {}
+
+        def quantise_streams(b):
+            vu_codes = work.tile([P, 2 * J], U32, tag="vu_codes", name="vu_codes", align_bytes=64)
+            vu_scales = work.tile([P, 2 * J], U8, tag="vu_scales", name="vu_scales", align_bytes=64)
+            nc.vector.quantize_mx(out=vu_codes[:].bitcast(FP8X4), scales=vu_scales[:], in_=grouped[b][:])
+            operands[b] = (vu_codes, vu_scales)
+
+        graph = {}
+
+        def graph_turned(b, cc):
+            vu_codes, vu_scales = operands[b]
+            y_turned = graph[b][1]
+            y_ps = psum_y.tile([P, K, J], F32, tag="y", name="y_ps")
+            for n in range(K):
+                ob = cc * K + n
+                nc.tensor.matmul_mx(
+                    out=y_ps[:, n, :],
+                    lhsT=wg_codes[:, ob * P : (ob + 1) * P].bitcast(FP8X4),
+                    lhsT_scale=wg_scales[:, ob * P : (ob + 1) * P],
+                    rhs=vu_codes[:, J : 2 * J].bitcast(FP8X4),
+                    rhs_scale=vu_scales[:, J : 2 * J],
+                    start=True,
+                    stop=True,
+                )
+            for n in range(K):
+                ob = cc * K + n
+                nc.scalar.activation(
+                    out=y_turned[:, ob * J : (ob + 1) * J].rearrange("p (m q) -> p m q", q=Q),
+                    in_=y_ps[:, n, :].rearrange("p (q m) -> p m q", q=Q),
+                    func=IDENTITY,
+                    bias=bias_col[:, ob : ob + 1],
+                )
+
+        def graph_direct(b, cc):
+            vu_codes, vu_scales = operands[b]
+            y_grp = graph[b][0]
+            y_ps = psum_y.tile([P, Q, CHUNK], F32, tag="y", name="y_ps")
+            w_cols = slice(cc * CHUNK, (cc + 1) * CHUNK)
+            n = DIRECT.index(cc)
+            for q in range(Q):
+                u_cols = slice(J + q * P, J + (q + 1) * P)
+                nc.tensor.matmul_mx(
+                    out=y_ps[:, q, :],
+                    lhsT=vu_codes[:, u_cols].bitcast(FP8X4),
+                    lhsT_scale=vu_scales[:, u_cols],
+                    rhs=wg_codes[:, w_cols].bitcast(FP8X4),
+                    rhs_scale=wg_scales[:, w_cols],
+                    start=True,
+                    stop=True,
+                )
+            nc.vector.tensor_tensor(
+                out=y_grp[:, cc * Q * CHUNK : (cc + 1) * Q * CHUNK].rearrange("p (o q) -> p o q", q=Q),
+                in0=y_ps[:].rearrange("p q o -> p o q"),
+                in1=gb_sb[:, n * CHUNK : (n + 1) * CHUNK].unsqueeze(2).to_broadcast([P, CHUNK, Q]),
+                op=ADD,
+            )
+
+        def begin_graph(b):
+            y_grp = work.tile([P, C * PACK], BF16, tag="y_grp", name="y_grp", align_bytes=64)
+            y_turned = work.tile([P, K * C * Q], BF16, tag="y_turned", name="y_turned")
+            graph[b] = (y_grp, y_turned)
+
+        def turn_graph(b):
+            y_grp, y_turned = graph[b]
+            words = y_turned[:].bitcast(F32)
+            group_words = y_grp[:].bitcast(F32)
+            for pair in (TURNED[0:2], TURNED[2:4]):
+                if pair:
+                    t_ps = psum_y.tile([P, len(pair) * CHUNK], F32, tag="y", name="t_ps")
+                    for n, cc in enumerate(pair):
+                        for half in range(K):
+                            col = cc * CHUNK + half * P
+                            nc.tensor.transpose(
+                                t_ps[:, n * CHUNK + half * P : n * CHUNK + (half + 1) * P],
+                                words[:, col : col + P],
+                                ident_f32[:],
+                            )
+                    first = pair[0] * CHUNK
+                    nc.scalar.copy(out=group_words[:, first : first + len(pair) * CHUNK], in_=t_ps[:])
+
+        def quantise_graph(b):
+            y_codes = work.tile([P, C], U32, tag="y_codes", name="y_codes", align_bytes=64)
+            y_scales = work.tile([P, C], U8, tag="y_scales", name="y_scales", align_bytes=64)
+            nc.vector.quantize_mx(out=y_codes[:].bitcast(FP8X4), scales=y_scales[:], in_=graph[b][0][:])
+            graph[b] = (y_codes, y_scales)
+
+        results = {}
+
+        def output_sums(b):
+            vu_codes, vu_scales = operands[b]
+            y_codes, y_scales = graph[b]
+            banks = []
+            for q in range(Q):
+                f_ps = psum_f.tile([P, C], F32, tag="f", name="f_ps")
+                cols = slice(q * P, (q + 1) * P)
+                nc.tensor.matmul_mx(
+                    out=f_ps[:],
+                    lhsT=vu_codes[:, cols].bitcast(FP8X4),
+                    lhsT_scale=vu_scales[:, cols],
+                    rhs=wp_codes[:].bitcast(FP8X4),
+                    rhs_scale=wp_scales[:],
+                    start=True,
+                    stop=False,
+                )
+                banks.append(f_ps)
+            for q in range(Q):
+                cols = slice(q * P, (q + 1) * P)
+                nc.tensor.matmul_mx(
+                    out=banks[q][:],
+                    lhsT=adj_codes[:, cols].bitcast(FP8X4),
+                    lhsT_scale=adj_scales[:, cols],
+                    rhs=y_codes[:].bitcast(FP8X4),
+                    rhs_scale=y_scales[:],
+                    start=False,
+                    stop=True,
+                )
+            results[b] = banks
+
+        def store(b):
+            xb = residual[b]
+            for q in range(Q):
+                cols = slice(q * C, (q + 1) * C)
+                nc.vector.tensor_tensor(out=xb[:, cols], in0=results[b][q][:], in1=xb[:, cols], op=ADD)
+            nc.sync.dma_start(out=out[b].rearrange("(p q) c -> p (q c)", q=Q), in_=xb[:])
+
+        fuse_streams(0)
+        turn_streams(0)
         wg_grp = staging.tile([P, K * C * PACK], BF16, name="wg_grp", align_bytes=64)
         wg_codes = consts.tile([P, K * C], U32, name="wg_codes", align_bytes=64)
         wg_scales = consts.tile([P, K * C], U8, name="wg_scales", align_bytes=64)
@@ -140,174 +324,69 @@ def tile_block_pb_t_kernel(tc, attn_o, xg1, x, adj, proj_w, proj_b, gcn2_w, gcn2
                     col = (cc * K + k) * C + t * P
                     nc.tensor.transpose(w_ps[:, t, k, :], wg_raw[:, col : col + P], ident_bf[:])
             chunk = wg_grp[:, cc * K * C : (cc + 1) * K * C]
-            grouped = chunk.rearrange("p (c k t) -> p c k t", k=K, t=PACK)
+            chunk_grouped = chunk.rearrange("p (c k t) -> p c k t", k=K, t=PACK)
             if cc % 2 == 0:
-                nc.scalar.copy(out=grouped, in_=w_ps[:].rearrange("p t k c -> p c k t"))
+                nc.scalar.copy(out=chunk_grouped, in_=w_ps[:].rearrange("p t k c -> p c k t"))
             else:
-                nc.vector.tensor_copy(out=grouped, in_=w_ps[:].rearrange("p t k c -> p c k t"))
-            cols = slice(cc * K * P, (cc + 1) * K * P)
+                nc.vector.tensor_copy(out=chunk_grouped, in_=w_ps[:].rearrange("p t k c -> p c k t"))
+            cols = slice(cc * CHUNK, (cc + 1) * CHUNK)
             nc.vector.quantize_mx(out=wg_codes[:, cols].bitcast(FP8X4), scales=wg_scales[:, cols], in_=chunk)
+        quantise_streams(0)
+        fuse_streams(1)
+        turn_streams(1)
 
+        wp_half = staging.tile([P, PACK * C], BF16, name="wp_half")
+        nc.vector.tensor_scalar(out=wp_half[:], in0=wp_raw[:], scalar1=0.5, scalar2=None, op0=MULT)
         wp_grp = staging.tile([P, C * PACK], BF16, name="wp_grp", align_bytes=64)
         wp_codes = consts.tile([P, C], U32, name="wp_codes", align_bytes=64)
         wp_scales = consts.tile([P, C], U8, name="wp_scales", align_bytes=64)
-        wp_words = wp_raw[:].bitcast(F32)
+        wp_words = wp_half[:].bitcast(F32)
         for hf in range(2):
             w_ps = psum_front.tile([P, 2, 2, P], F32, tag="front", name="wp_ps")
-            for u in range(2):
+            for w in range(2):
                 for o2 in range(2):
-                    col = (hf * 2 + o2) * (C // 2) + u * P
-                    nc.tensor.transpose(w_ps[:, u, o2, :], wp_words[:, col : col + P], ident_f32[:])
+                    col = (hf * 2 + o2) * (C // 2) + w * P
+                    nc.tensor.transpose(w_ps[:, w, o2, :], wp_words[:, col : col + P], ident_f32[:])
             nc.scalar.copy(
-                out=wp_grp[:].bitcast(F32)[:, hf * C : (hf + 1) * C].rearrange("q (o u) -> q o u", u=2),
-                in_=w_ps[:].rearrange("q u o2 o -> q (o2 o) u"),
+                out=wp_grp[:].bitcast(F32)[:, hf * C : (hf + 1) * C].rearrange("p (o w) -> p o w", w=2),
+                in_=w_ps[:].rearrange("p w o2 o -> p (o2 o) w"),
             )
         nc.vector.quantize_mx(out=wp_codes[:].bitcast(FP8X4), scales=wp_scales[:], in_=wp_grp[:])
 
         adj_grp = staging.tile([P, J * PACK], BF16, name="adj_grp", align_bytes=64)
         adj_codes = consts.tile([P, J], U32, name="adj_codes", align_bytes=64)
         adj_scales = consts.tile([P, J], U8, name="adj_scales", align_bytes=64)
-        adj_view = adj_raw[:].rearrange("p (k jh mw wh) -> p wh mw jh k", k=K, jh=TILES, wh=TILES)
-        for wh in range(TILES):
+        adj_view = adj_raw[:].rearrange("p (k q mw wh) -> p wh mw k q", k=K, q=Q, wh=Q)
+        for wh in range(Q):
             nc.vector.tensor_copy(
-                out=adj_grp[:, wh * C : (wh + 1) * C].rearrange("p (mw jh k) -> p mw jh k", jh=TILES, k=K),
+                out=adj_grp[:, wh * C : (wh + 1) * C].rearrange("p (mw k q) -> p mw k q", k=K, q=Q),
                 in_=adj_view[:, wh],
             )
         nc.vector.quantize_mx(out=adj_codes[:].bitcast(FP8X4), scales=adj_scales[:], in_=adj_grp[:])
 
-        fused = {}
-
-        def transpose_and_combine(b):
-            ag = stacked[b]
-            ag_words = ag[:].bitcast(F32)
-            a_sb = work.tile([P, J * PACK], BF16, tag="a_sb", name="a_sb")
-            g_sb = work.tile([P, J * PACK], BF16, tag="g_sb", name="g_sb")
-            h_sb = work.tile([P, J * PACK], BF16, tag="h_sb", name="h_sb")
-            vu_grp = work.tile([P, 2 * J * PACK], BF16, tag="vu_grp", name="vu_grp", align_bytes=64)
-            a_words = a_sb[:].bitcast(F32).rearrange("q (wh mh i u) -> q wh mh i u", wh=TILES, mh=2, u=2)
-            g_words = g_sb[:].bitcast(F32).rearrange("q (wh mh i u) -> q wh mh i u", wh=TILES, mh=2, u=2)
-            for wh in range(TILES):
-                t_ps = psum_front.tile([P, 2, 2, P], F32, tag="front", name="t_ps")
-                for u in range(2):
-                    for mh in range(2):
-                        col = (2 * mh + wh) * (C // 2) + u * P
-                        nc.tensor.transpose(t_ps[:, u, mh, :], ag_words[:, col : col + P], ident_f32[:])
-                split = t_ps[:].rearrange("q u mh (i s) -> q s mh i u", s=2)
-                nc.scalar.copy(out=a_words[:, wh], in_=split[:, 0])
-                nc.scalar.copy(out=g_words[:, wh], in_=split[:, 1])
-            for jh in range(TILES):
-                u_ps = psum_front.tile([P, PACK, P], F32, tag="front", name="u_ps")
-                for t in range(PACK):
-                    for mh in range(2):
-                        col = (2 * mh + jh) * C + t * P
-                        nc.tensor.matmul(
-                            u_ps[:, t, mh * HALF : (mh + 1) * HALF],
-                            lhsT=ag[:, col : col + P],
-                            rhs=combine[:],
-                            start=True,
-                            stop=True,
-                        )
-                first = (TILES + jh) * P * PACK
-                nc.scalar.activation(
-                    out=vu_grp[:, first : first + P * PACK].rearrange("p (m t) -> p m t", t=PACK),
-                    in_=u_ps[:].rearrange("p t m -> p m t"),
-                    func=COPY,
-                    scale=S_A2G,
-                )
-            nc.scalar.activation(out=h_sb[:], in_=g_sb[:], func=COPY, scale=S_G2A)
-            fused[b] = (a_sb, h_sb, vu_grp)
-
-        operands = {}
-
-        def quantise_streams(b):
-            a_sb, h_sb, vu_grp = fused[b]
-            nc.vector.tensor_tensor(out=vu_grp[:, 0 : J * PACK], in0=a_sb[:], in1=h_sb[:], op=ADD)
-            vu_codes = work.tile([P, 2 * J], U32, tag="vu_codes", name="vu_codes", align_bytes=64)
-            vu_scales = work.tile([P, 2 * J], U8, tag="vu_scales", name="vu_scales", align_bytes=64)
-            nc.vector.quantize_mx(out=vu_codes[:].bitcast(FP8X4), scales=vu_scales[:], in_=vu_grp[:])
-            operands[b] = (vu_codes, vu_scales)
-
-        graph = {}
-
-        def graph_linear(b):
-            vu_codes, vu_scales = operands[b]
-            y_grp = work.tile([P, C * PACK], BF16, tag="y_grp", name="y_grp", align_bytes=64)
-            for cc in range(PACK):
-                y_ps = psum_y.tile([P, TILES, K * P], F32, tag="y", name="y_ps")
-                w_cols = slice(cc * K * P, (cc + 1) * K * P)
-                for jh in range(TILES):
-                    u_cols = slice((TILES + jh) * P, (TILES + jh + 1) * P)
-                    nc.tensor.matmul_mx(
-                        out=y_ps[:, jh, :],
-                        lhsT=vu_codes[:, u_cols].bitcast(FP8X4),
-                        lhsT_scale=vu_scales[:, u_cols],
-                        rhs=wg_codes[:, w_cols].bitcast(FP8X4),
-                        rhs_scale=wg_scales[:, w_cols],
-                        start=True,
-                        stop=True,
-                    )
-                nc.vector.tensor_tensor(
-                    out=y_grp[:, cc * C : (cc + 1) * C].rearrange("p (c jh k) -> p c jh k", jh=TILES, k=K),
-                    in0=y_ps[:].rearrange("p jh (c k) -> p c jh k", k=K),
-                    in1=gb_sb[:, w_cols].rearrange("p (c k) -> p c k", k=K).unsqueeze(2).to_broadcast([P, P, TILES, K]),
-                    op=ADD,
-                )
-            graph[b] = y_grp
-
-        sums = {}
-
-        def open_output_sums(b):
-            vu_codes, vu_scales = operands[b]
-            banks = []
-            for wh in range(TILES):
-                f_ps = psum_f.tile([P, C], F32, tag="f", name="f_ps")
-                v_cols = slice(wh * P, (wh + 1) * P)
-                nc.tensor.matmul_mx(
-                    out=f_ps[:],
-                    lhsT=vu_codes[:, v_cols].bitcast(FP8X4),
-                    lhsT_scale=vu_scales[:, v_cols],
-                    rhs=wp_codes[:].bitcast(FP8X4),
-                    rhs_scale=wp_scales[:],
-                    start=True,
-                    stop=False,
-                )
-                banks.append(f_ps)
-            sums[b] = banks
-
-        def quantise_graph(b):
-            y_codes = work.tile([P, C], U32, tag="y_codes", name="y_codes", align_bytes=64)
-            y_scales = work.tile([P, C], U8, tag="y_scales", name="y_scales", align_bytes=64)
-            nc.vector.quantize_mx(out=y_codes[:].bitcast(FP8X4), scales=y_scales[:], in_=graph[b][:])
-            graph[b] = (y_codes, y_scales)
-
-        def aggregate_and_store(b):
-            y_codes, y_scales = graph[b]
-            xb = residual[b]
-            for wh in range(TILES):
-                w_cols = slice(wh * P, (wh + 1) * P)
-                nc.tensor.matmul_mx(
-                    out=sums[b][wh][:],
-                    lhsT=adj_codes[:, w_cols].bitcast(FP8X4),
-                    lhsT_scale=adj_scales[:, w_cols],
-                    rhs=y_codes[:].bitcast(FP8X4),
-                    rhs_scale=y_scales[:],
-                    start=False,
-                    stop=True,
-                )
-            for wh in range(TILES):
-                cols = slice(wh * C, (wh + 1) * C)
-                nc.vector.tensor_tensor(out=xb[:, cols], in0=sums[b][wh][:], in1=xb[:, cols], op=ADD)
-            nc.sync.dma_start(out=out[b].rearrange("(m wh) c -> m (wh c)", wh=TILES), in_=xb[:])
-
-        transpose_and_combine(0)
-        quantise_streams(0)
-        transpose_and_combine(1)
-        for b in range(B):
-            graph_linear(b)
-            open_output_sums(b)
+        fuse_streams(2)
+        for b in range(B + 1):
+            if b + AHEAD < B:
+                load_streams(b + AHEAD)
+                load_residual(b + AHEAD)
+            if b > 0:
+                quantise_graph(b - 1)
+                add_proj_bias(b - 1)
+            if b < B:
+                begin_graph(b)
+                for cc in TURNED:
+                    graph_turned(b, cc)
+                for cc in DIRECT:
+                    graph_direct(b, cc)
+            if b > 0:
+                output_sums(b - 1)
             if b + 2 < B:
-                transpose_and_combine(b + 2)
-            quantise_graph(b)
+                turn_streams(b + 2)
+            if b < B:
+                turn_graph(b)
             if b + 1 < B:
                 quantise_streams(b + 1)
-            aggregate_and_store(b)
+            if b > 0:
+                store(b - 1)
+            if b + 3 < B:
+                fuse_streams(b + 3)

@@ -11,6 +11,7 @@ U8 = mybir.dt.uint8
 ADD = mybir.AluOpType.add
 MULT = mybir.AluOpType.mult
 COPY = mybir.ActivationFunctionType.Copy
+ENGINES = mybir.EngineType
 IDENTITY = mybir.ActivationFunctionType.Identity
 
 B, J, C, K, H = 16, 256, 512, 2, 8
@@ -18,6 +19,7 @@ DH = C // H
 P = 128
 PACK = 4
 Q = J // P
+LATE = 96
 AHEAD = 6
 CHUNK = K * P
 DIRECT = (3,)
@@ -34,10 +36,14 @@ def tile_block_pb_t_kernel(tc, attn_o, xg1, x, adj, proj_w, proj_b, gcn2_w, gcn2
         loads = stack.enter_context(tc.tile_pool(name="loads", bufs=8))
         sums = stack.enter_context(tc.tile_pool(name="sums", bufs=8))
         work = stack.enter_context(tc.tile_pool(name="work", bufs=3))
-        psum_front = stack.enter_context(tc.psum_pool(name="psum_front", bufs=3))
-        psum_y = stack.enter_context(tc.psum_pool(name="psum_y", bufs=3))
+        psum_s = stack.enter_context(tc.psum_pool(name="psum_s", bufs=5))
+        psum_d = stack.enter_context(tc.psum_pool(name="psum_d", bufs=1))
         psum_f = stack.enter_context(tc.psum_pool(name="psum_f", bufs=2))
 
+        bias_row = consts.tile([P, K * C + C], BF16, name="bias_row")
+        nc.vector.memset(bias_row[:], 0.0)
+        nc.scalar.dma_start(out=bias_row[0:1, 0 : K * C], in_=gcn2_b.unsqueeze(0))
+        nc.scalar.dma_start(out=bias_row[0:1, K * C : K * C + C], in_=proj_b.unsqueeze(0))
         ident_f32 = consts.tile([P, P], F32, name="ident_f32")
         make_identity(nc, ident_f32[:])
         ident_bf = consts.tile([P, P], BF16, name="ident_bf")
@@ -46,11 +52,6 @@ def tile_block_pb_t_kernel(tc, attn_o, xg1, x, adj, proj_w, proj_b, gcn2_w, gcn2
         nc.vector.tensor_scalar(out=ident_25[:], in0=ident_bf[:], scalar1=2.5, scalar2=None, op0=MULT)
         ones = consts.tile([P, P], BF16, name="ones")
         nc.vector.memset(ones[:], 1.0)
-
-        bias_row = consts.tile([P, K * C + C], BF16, name="bias_row")
-        nc.vector.memset(bias_row[:], 0.0)
-        nc.scalar.dma_start(out=bias_row[0:1, 0 : K * C], in_=gcn2_b.unsqueeze(0))
-        nc.scalar.dma_start(out=bias_row[0:1, K * C : K * C + C], in_=proj_b.unsqueeze(0))
 
         wg_raw = staging.tile([P, PACK * K * C], BF16, name="wg_raw")
         wg_rows = gcn2_w.rearrange("(k cc p) c -> cc p k c", k=K, cc=PACK)
@@ -78,9 +79,8 @@ def tile_block_pb_t_kernel(tc, attn_o, xg1, x, adj, proj_w, proj_b, gcn2_w, gcn2
             nc.sync.dma_start(out=x_sb[:], in_=x[b].rearrange("(p q) c -> p (q c)", q=Q))
             residual_in[b] = x_sb
 
-        load_gcn_weight_chunk(0)
         load_streams(0)
-        for cc in range(1, PACK):
+        for cc in range(PACK):
             load_gcn_weight_chunk(cc)
         load_streams(1)
         adj_raw = staging.tile([P, K * Q * J], BF16, name="adj_raw")
@@ -92,46 +92,52 @@ def tile_block_pb_t_kernel(tc, attn_o, xg1, x, adj, proj_w, proj_b, gcn2_w, gcn2
             out=wp_raw[:].rearrange("p (ot c) -> p ot c", ot=PACK), in_=proj_w.rearrange("(ot p) c -> p ot c", p=P)
         )
         load_streams(2)
-        for b in range(AHEAD):
+        for b in range(AHEAD + 1):
             load_residual(b)
-            if b + 3 < AHEAD:
+            if b + 3 <= AHEAD:
                 load_streams(b + 3)
 
         bias_pairs = consts.tile([P, K * C], BF16, name="bias_pairs")
-        nc.vector.tensor_copy(
-            out=bias_pairs[:].rearrange("p (c k) -> p c k", k=K),
-            in_=bias_row[:, 0 : K * C].rearrange("p (k c) -> p c k", k=K),
-        )
         bias_col = consts.tile([P, K * PACK], F32, name="bias_col")
-        c_ps = psum_front.tile([P, K * PACK, 2], F32, tag="front", name="c_ps")
-        for ob in range(K * PACK):
-            nc.tensor.matmul(
-                c_ps[:, ob, :], lhsT=bias_pairs[:, ob * P : (ob + 1) * P], rhs=ones[:, 0:2], start=True, stop=True
-            )
-        nc.vector.tensor_copy(out=bias_col[:].unsqueeze(2), in_=c_ps[:, :, 0:1])
         gb_sb = consts.tile([P, len(DIRECT) * CHUNK], F32, name="gb_sb")
-        for n, cc in enumerate(DIRECT):
-            g_ps = psum_front.tile([P, CHUNK], F32, tag="front", name="g_ps")
-            nc.tensor.matmul(
-                g_ps[:], lhsT=ones[:], rhs=bias_pairs[:, cc * CHUNK : (cc + 1) * CHUNK], start=True, stop=True
-            )
-            nc.vector.tensor_copy(out=gb_sb[:, n * CHUNK : (n + 1) * CHUNK], in_=g_ps[:])
         pb_sb = consts.tile([P, C], F32, name="pb_sb")
-        p_ps = psum_front.tile([P, C], F32, tag="front", name="p_ps")
-        nc.tensor.matmul(p_ps[:], lhsT=ones[:], rhs=bias_row[:, K * C : K * C + C], start=True, stop=True)
-        nc.vector.tensor_copy(out=pb_sb[:], in_=p_ps[:])
+
+        def spread_biases():
+            nc.vector.tensor_copy(
+                out=bias_pairs[:].rearrange("p (c k) -> p c k", k=K),
+                in_=bias_row[:, 0 : K * C].rearrange("p (k c) -> p c k", k=K),
+            )
+            p_ps = psum_s.tile([P, C], F32, tag="s", name="p_ps")
+            nc.tensor.matmul(p_ps[:], lhsT=ones[:], rhs=bias_row[:, K * C : K * C + C], start=True, stop=True)
+            nc.scalar.copy(out=pb_sb[:], in_=p_ps[:])
+            c_ps = psum_s.tile([P, K * PACK, 2], F32, tag="s", name="c_ps")
+            for ob in range(K * PACK):
+                nc.tensor.matmul(
+                    c_ps[:, ob, :], lhsT=bias_pairs[:, ob * P : (ob + 1) * P], rhs=ones[:, 0:2], start=True, stop=True
+                )
+            nc.scalar.copy(out=bias_col[:].unsqueeze(2), in_=c_ps[:, :, 0:1])
+            for n, cc in enumerate(DIRECT):
+                g_ps = psum_s.tile([P, CHUNK], F32, tag="s", name="g_ps")
+                nc.tensor.matmul(
+                    g_ps[:], lhsT=ones[:], rhs=bias_pairs[:, cc * CHUNK : (cc + 1) * CHUNK], start=True, stop=True
+                )
+                nc.scalar.copy(out=gb_sb[:, n * CHUNK : (n + 1) * CHUNK], in_=g_ps[:])
 
         residual = {}
 
         def add_proj_bias(b):
             xb = sums.tile([P, Q * C], F32, tag="xb", name="xb")
-            nc.gpsimd.tensor_tensor(out=xb[:, 0:C], in0=residual_in[b][:, 0:C], in1=pb_sb[:], op=ADD)
-            nc.vector.tensor_tensor(out=xb[:, C : 2 * C], in0=residual_in[b][:, C : 2 * C], in1=pb_sb[:], op=ADD)
+            nc.vector.tensor_tensor(
+                out=xb[:, C + LATE : 2 * C], in0=residual_in[b][:, C + LATE : 2 * C], in1=pb_sb[:, LATE:C], op=ADD
+            )
             residual[b] = xb
 
         natural = {}
 
-        def fuse_streams(b):
+        def plain_tiles(b):
+            return (0, 1) if b % 2 else (0,)
+
+        def double_attention(b):
             a_raw, g_raw = streams[b]
             a2 = work.tile([P, Q * C], BF16, tag="a2", name="a2")
             nc.vector.tensor_scalar(
@@ -141,12 +147,18 @@ def tile_block_pb_t_kernel(tc, attn_o, xg1, x, adj, proj_w, proj_b, gcn2_w, gcn2
                 scalar2=None,
                 op0=MULT,
             )
-            u_nat = work.tile([P, C], BF16, tag="u_nat", name="u_nat")
-            nc.vector.scalar_tensor_tensor(
-                out=u_nat[:], in0=a2[:, C : 2 * C], scalar=0.4, in1=g_raw[:, C : 2 * C], op0=MULT, op1=ADD
-            )
+            natural[b] = (a2, g_raw)
+
+        def fuse_streams(b):
+            a2, g_raw = natural[b]
             v_nat = work.tile([P, Q * C], BF16, tag="v_nat", name="v_nat")
             nc.vector.tensor_tensor(out=v_nat[:], in0=a2[:], in1=g_raw[:], op=ADD)
+            u_nat = None
+            if 1 not in plain_tiles(b):
+                u_nat = work.tile([P, C], BF16, tag="u_nat", name="u_nat")
+                nc.vector.scalar_tensor_tensor(
+                    out=u_nat[:], in0=a2[:, C : 2 * C], scalar=0.4, in1=g_raw[:, C : 2 * C], op0=MULT, op1=ADD
+                )
             natural[b] = (a2, g_raw, u_nat, v_nat)
 
         grouped = {}
@@ -155,7 +167,7 @@ def tile_block_pb_t_kernel(tc, attn_o, xg1, x, adj, proj_w, proj_b, gcn2_w, gcn2
             a2, g_raw, u_nat, v_nat = natural[b]
             vu_grp = work.tile([P, 2 * J * PACK], BF16, tag="vu_grp", name="vu_grp", align_bytes=64)
             v_words = v_nat[:].bitcast(F32)
-            v_ps = psum_front.tile([P, Q, 2, P], F32, tag="front", name="v_ps")
+            v_ps = psum_s.tile([P, Q, 2, P], F32, tag="s", name="v_ps")
             for q in range(Q):
                 for w in range(2):
                     col = (2 * q + w) * P
@@ -164,26 +176,21 @@ def tile_block_pb_t_kernel(tc, attn_o, xg1, x, adj, proj_w, proj_b, gcn2_w, gcn2
                 out=vu_grp[:].bitcast(F32)[:, 0 : J * 2].rearrange("p (q m w) -> p q m w", q=Q, w=2),
                 in_=v_ps[:].rearrange("p q w m -> p q m w"),
             )
-            u_ps = psum_front.tile([P, PACK, P], BF16, tag="front", name="u_ps")
-            for t in range(PACK):
-                nc.tensor.transpose(u_ps[:, t, :], u_nat[:, t * P : (t + 1) * P], ident_bf[:])
-            first = (J + P) * PACK
-            nc.scalar.copy(
-                out=vu_grp[:, first : first + P * PACK].rearrange("p (m t) -> p m t", t=PACK),
-                in_=u_ps[:].rearrange("p t m -> p m t"),
-            )
-            s_ps = psum_front.tile([P, PACK, P], F32, tag="front", name="s_ps")
-            for t in range(PACK):
-                cols = slice(t * P, (t + 1) * P)
-                nc.tensor.matmul(s_ps[:, t, :], lhsT=a2[:, cols], rhs=ident_bf[:], start=True, stop=False)
-                nc.tensor.matmul(s_ps[:, t, :], lhsT=g_raw[:, cols], rhs=ident_25[:], start=False, stop=True)
-            first = J * PACK
-            nc.scalar.activation(
-                out=vu_grp[:, first : first + P * PACK].rearrange("p (m t) -> p m t", t=PACK),
-                in_=s_ps[:].rearrange("p t m -> p m t"),
-                func=COPY,
-                scale=0.4,
-            )
+            for q in range(Q):
+                first = (J + q * P) * PACK
+                u_out = vu_grp[:, first : first + P * PACK].rearrange("p (m t) -> p m t", t=PACK)
+                if q in plain_tiles(b):
+                    s_ps = psum_s.tile([P, PACK, P], F32, tag="s", name="s_ps")
+                    for t in range(PACK):
+                        cols = slice(q * C + t * P, q * C + (t + 1) * P)
+                        nc.tensor.matmul(s_ps[:, t, :], lhsT=a2[:, cols], rhs=ident_bf[:], start=True, stop=False)
+                        nc.tensor.matmul(s_ps[:, t, :], lhsT=g_raw[:, cols], rhs=ident_25[:], start=False, stop=True)
+                    nc.scalar.activation(out=u_out, in_=s_ps[:].rearrange("p t m -> p m t"), func=COPY, scale=0.4)
+                else:
+                    u_ps = psum_s.tile([P, PACK, P], BF16, tag="s", name="u_ps")
+                    for t in range(PACK):
+                        nc.tensor.transpose(u_ps[:, t, :], u_nat[:, t * P : (t + 1) * P], ident_bf[:])
+                    nc.scalar.copy(out=u_out, in_=u_ps[:].rearrange("p t m -> p m t"))
             grouped[b] = vu_grp
 
         operands = {}
@@ -195,11 +202,12 @@ def tile_block_pb_t_kernel(tc, attn_o, xg1, x, adj, proj_w, proj_b, gcn2_w, gcn2
             operands[b] = (vu_codes, vu_scales)
 
         graph = {}
+        direct_sums = {}
 
         def graph_turned(b, cc):
             vu_codes, vu_scales = operands[b]
             y_turned = graph[b][1]
-            y_ps = psum_y.tile([P, K, J], F32, tag="y", name="y_ps")
+            y_ps = psum_s.tile([P, K, J], F32, tag="s", name="y_ps")
             for n in range(K):
                 ob = cc * K + n
                 nc.tensor.matmul_mx(
@@ -222,10 +230,8 @@ def tile_block_pb_t_kernel(tc, attn_o, xg1, x, adj, proj_w, proj_b, gcn2_w, gcn2
 
         def graph_direct(b, cc):
             vu_codes, vu_scales = operands[b]
-            y_grp = graph[b][0]
-            y_ps = psum_y.tile([P, Q, CHUNK], F32, tag="y", name="y_ps")
+            y_ps = psum_d.tile([P, Q, CHUNK], F32, tag="d", name="y_ps")
             w_cols = slice(cc * CHUNK, (cc + 1) * CHUNK)
-            n = DIRECT.index(cc)
             for q in range(Q):
                 u_cols = slice(J + q * P, J + (q + 1) * P)
                 nc.tensor.matmul_mx(
@@ -237,6 +243,12 @@ def tile_block_pb_t_kernel(tc, attn_o, xg1, x, adj, proj_w, proj_b, gcn2_w, gcn2
                     start=True,
                     stop=True,
                 )
+            direct_sums[b, cc] = y_ps
+
+        def add_direct_bias(b, cc):
+            y_grp = graph[b][0]
+            y_ps = direct_sums[b, cc]
+            n = DIRECT.index(cc)
             nc.vector.tensor_tensor(
                 out=y_grp[:, cc * Q * CHUNK : (cc + 1) * Q * CHUNK].rearrange("p (o q) -> p o q", q=Q),
                 in0=y_ps[:].rearrange("p q o -> p o q"),
@@ -255,7 +267,7 @@ def tile_block_pb_t_kernel(tc, attn_o, xg1, x, adj, proj_w, proj_b, gcn2_w, gcn2
             group_words = y_grp[:].bitcast(F32)
             for pair in (TURNED[0:2], TURNED[2:4]):
                 if pair:
-                    t_ps = psum_y.tile([P, len(pair) * CHUNK], F32, tag="y", name="t_ps")
+                    t_ps = psum_s.tile([P, len(pair) * CHUNK], F32, tag="s", name="t_ps")
                     for n, cc in enumerate(pair):
                         for half in range(K):
                             col = cc * CHUNK + half * P
@@ -305,88 +317,149 @@ def tile_block_pb_t_kernel(tc, attn_o, xg1, x, adj, proj_w, proj_b, gcn2_w, gcn2
                 )
             results[b] = banks
 
+        def add_residual(b):
+            xb = residual[b]
+            for q, width in ((1, LATE), (0, C)):
+                cols = slice(q * C, q * C + width)
+                nc.vector.tensor_tensor(out=xb[:, cols], in0=results[b][q][:, 0:width], in1=residual_in[b][:, cols], op=ADD)
+                nc.gpsimd.tensor_tensor(out=xb[:, cols], in0=xb[:, cols], in1=pb_sb[:, 0:width], op=ADD)
+            cols = slice(C + LATE, 2 * C)
+            nc.vector.tensor_tensor(out=xb[:, cols], in0=results[b][1][:, LATE:C], in1=xb[:, cols], op=ADD)
+
         def store(b):
             xb = residual[b]
-            for q in range(Q):
-                cols = slice(q * C, (q + 1) * C)
-                nc.vector.tensor_tensor(out=xb[:, cols], in0=results[b][q][:], in1=xb[:, cols], op=ADD)
             nc.sync.dma_start(out=out[b].rearrange("(p q) c -> p (q c)", q=Q), in_=xb[:])
 
-        fuse_streams(0)
-        turn_streams(0)
         wg_grp = staging.tile([P, K * C * PACK], BF16, name="wg_grp", align_bytes=64)
         wg_codes = consts.tile([P, K * C], U32, name="wg_codes", align_bytes=64)
         wg_scales = consts.tile([P, K * C], U8, name="wg_scales", align_bytes=64)
-        for cc in range(PACK):
-            w_ps = psum_y.tile([P, PACK, K, P], BF16, tag="y", name="w_ps")
+
+        def turn_gcn_weight(cc, copy):
+            w_ps = psum_s.tile([P, PACK, K, P], BF16, tag="s", name="w_ps")
             for t in range(PACK):
                 for k in range(K):
                     col = (cc * K + k) * C + t * P
                     nc.tensor.transpose(w_ps[:, t, k, :], wg_raw[:, col : col + P], ident_bf[:])
             chunk = wg_grp[:, cc * K * C : (cc + 1) * K * C]
-            chunk_grouped = chunk.rearrange("p (c k t) -> p c k t", k=K, t=PACK)
-            if cc % 2 == 0:
-                nc.scalar.copy(out=chunk_grouped, in_=w_ps[:].rearrange("p t k c -> p c k t"))
-            else:
-                nc.vector.tensor_copy(out=chunk_grouped, in_=w_ps[:].rearrange("p t k c -> p c k t"))
+            copy(
+                out=chunk.rearrange("p (c k t) -> p c k t", k=K, t=PACK), in_=w_ps[:].rearrange("p t k c -> p c k t")
+            )
+
+        def quantise_gcn_weight(cc):
             cols = slice(cc * CHUNK, (cc + 1) * CHUNK)
+            chunk = wg_grp[:, cc * K * C : (cc + 1) * K * C]
             nc.vector.quantize_mx(out=wg_codes[:, cols].bitcast(FP8X4), scales=wg_scales[:, cols], in_=chunk)
-        quantise_streams(0)
-        fuse_streams(1)
-        turn_streams(1)
 
         wp_half = staging.tile([P, PACK * C], BF16, name="wp_half")
-        nc.vector.tensor_scalar(out=wp_half[:], in0=wp_raw[:], scalar1=0.5, scalar2=None, op0=MULT)
         wp_grp = staging.tile([P, C * PACK], BF16, name="wp_grp", align_bytes=64)
         wp_codes = consts.tile([P, C], U32, name="wp_codes", align_bytes=64)
         wp_scales = consts.tile([P, C], U8, name="wp_scales", align_bytes=64)
-        wp_words = wp_half[:].bitcast(F32)
-        for hf in range(2):
-            w_ps = psum_front.tile([P, 2, 2, P], F32, tag="front", name="wp_ps")
-            for w in range(2):
-                for o2 in range(2):
-                    col = (hf * 2 + o2) * (C // 2) + w * P
-                    nc.tensor.transpose(w_ps[:, w, o2, :], wp_words[:, col : col + P], ident_f32[:])
-            nc.scalar.copy(
-                out=wp_grp[:].bitcast(F32)[:, hf * C : (hf + 1) * C].rearrange("p (o w) -> p o w", w=2),
-                in_=w_ps[:].rearrange("p w o2 o -> p (o2 o) w"),
-            )
-        nc.vector.quantize_mx(out=wp_codes[:].bitcast(FP8X4), scales=wp_scales[:], in_=wp_grp[:])
+
+        def halve_proj_weight():
+            nc.vector.tensor_scalar(out=wp_half[:], in0=wp_raw[:], scalar1=0.5, scalar2=None, op0=MULT)
+
+        def turn_proj_weight():
+            wp_words = wp_half[:].bitcast(F32)
+            for hf in range(2):
+                w_ps = psum_s.tile([P, 2, 2, P], F32, tag="s", name="wp_ps")
+                for w in range(2):
+                    for o2 in range(2):
+                        col = (hf * 2 + o2) * (C // 2) + w * P
+                        nc.tensor.transpose(w_ps[:, w, o2, :], wp_words[:, col : col + P], ident_f32[:])
+                nc.scalar.copy(
+                    out=wp_grp[:].bitcast(F32)[:, hf * C : (hf + 1) * C].rearrange("p (o w) -> p o w", w=2),
+                    in_=w_ps[:].rearrange("p w o2 o -> p (o2 o) w"),
+                )
+
+        def quantise_proj_weight():
+            nc.vector.quantize_mx(out=wp_codes[:].bitcast(FP8X4), scales=wp_scales[:], in_=wp_grp[:])
 
         adj_grp = staging.tile([P, J * PACK], BF16, name="adj_grp", align_bytes=64)
         adj_codes = consts.tile([P, J], U32, name="adj_codes", align_bytes=64)
         adj_scales = consts.tile([P, J], U8, name="adj_scales", align_bytes=64)
-        adj_view = adj_raw[:].rearrange("p (k q mw wh) -> p wh mw k q", k=K, q=Q, wh=Q)
-        for wh in range(Q):
-            nc.vector.tensor_copy(
-                out=adj_grp[:, wh * C : (wh + 1) * C].rearrange("p (mw k q) -> p mw k q", k=K, q=Q),
-                in_=adj_view[:, wh],
-            )
-        nc.vector.quantize_mx(out=adj_codes[:].bitcast(FP8X4), scales=adj_scales[:], in_=adj_grp[:])
 
+        def group_adjacency():
+            adj_view = adj_raw[:].rearrange("p (k q mw wh) -> p wh mw k q", k=K, q=Q, wh=Q)
+            for wh in range(Q):
+                nc.vector.tensor_copy(
+                    out=adj_grp[:, wh * C : (wh + 1) * C].rearrange("p (mw k q) -> p mw k q", k=K, q=Q),
+                    in_=adj_view[:, wh],
+                )
+
+        def quantise_adjacency():
+            nc.vector.quantize_mx(out=adj_codes[:].bitcast(FP8X4), scales=adj_scales[:], in_=adj_grp[:])
+
+        stack.enter_context(tc.manual_schedule(engines={ENGINES.PE, ENGINES.DVE, ENGINES.Activation, ENGINES.Pool}))
+        spread_biases()
+        double_attention(0)
+        fuse_streams(0)
+        turn_streams(0)
+        turn_gcn_weight(0, nc.vector.tensor_copy)
+        turn_gcn_weight(1, nc.scalar.copy)
+        quantise_streams(0)
+        quantise_gcn_weight(0)
+        turn_gcn_weight(2, nc.vector.tensor_copy)
+        quantise_gcn_weight(1)
+        turn_gcn_weight(3, nc.scalar.copy)
+        double_attention(1)
+        quantise_gcn_weight(2)
+        quantise_gcn_weight(3)
+
+        begin_graph(0)
+        for cc in TURNED:
+            graph_turned(0, cc)
+        for cc in DIRECT:
+            graph_direct(0, cc)
+        fuse_streams(1)
+        for cc in DIRECT:
+            add_direct_bias(0, cc)
+        turn_streams(1)
+        turn_graph(0)
+        double_attention(2)
+        halve_proj_weight()
+        quantise_streams(1)
         fuse_streams(2)
-        for b in range(B + 1):
+        group_adjacency()
+        turn_proj_weight()
+        turn_streams(2)
+        quantise_adjacency()
+        quantise_proj_weight()
+        double_attention(3)
+        fuse_streams(3)
+        turn_streams(3)
+
+        for b in range(1, B + 1):
             if b + AHEAD < B:
                 load_streams(b + AHEAD)
                 load_residual(b + AHEAD)
-            if b > 0:
-                quantise_graph(b - 1)
-                add_proj_bias(b - 1)
             if b < B:
                 begin_graph(b)
+            if b < B:
                 for cc in TURNED:
                     graph_turned(b, cc)
-                for cc in DIRECT:
-                    graph_direct(b, cc)
-            if b > 0:
-                output_sums(b - 1)
-            if b + 2 < B:
-                turn_streams(b + 2)
-            if b < B:
-                turn_graph(b)
+            if b + 3 < B:
+                double_attention(b + 3)
+            if True:
+                quantise_graph(b - 1)
             if b + 1 < B:
                 quantise_streams(b + 1)
-            if b > 0:
-                store(b - 1)
+            if True:
+                output_sums(b - 1)
+            if b < B:
+                for cc in DIRECT:
+                    graph_direct(b, cc)
             if b + 3 < B:
                 fuse_streams(b + 3)
+            if True:
+                add_proj_bias(b - 1)
+            if True:
+                add_residual(b - 1)
+            if True:
+                store(b - 1)
+            if b < B:
+                for cc in DIRECT:
+                    add_direct_bias(b, cc)
+            if b < B:
+                turn_graph(b)
+            if b + 3 < B:
+                turn_streams(b + 3)

@@ -19,11 +19,11 @@ DH = C // H
 P = 128
 PACK = 4
 Q = J // P
-LATE = 96
 AHEAD = 6
 CHUNK = K * P
-DIRECT = (3,)
-TURNED = tuple(cc for cc in range(PACK) if cc not in DIRECT)
+DIRECT = (2, 3)
+
+NODIRECT = ()
 
 FLOPS = 2 * B * J * C * (C + K * C) + 2 * B * J * (K * J) * C
 
@@ -125,11 +125,15 @@ def tile_block_pb_t_kernel(tc, attn_o, xg1, x, adj, proj_w, proj_b, gcn2_w, gcn2
 
         residual = {}
 
+        def late_tiles(b):
+            return (0,) if b + 2 < B else ()
+
         def add_proj_bias(b):
             xb = sums.tile([P, Q * C], F32, tag="xb", name="xb")
-            nc.vector.tensor_tensor(
-                out=xb[:, C + LATE : 2 * C], in0=residual_in[b][:, C + LATE : 2 * C], in1=pb_sb[:, LATE:C], op=ADD
-            )
+            for q in range(Q):
+                if q not in late_tiles(b):
+                    cols = slice(q * C, (q + 1) * C)
+                    nc.vector.tensor_tensor(out=xb[:, cols], in0=residual_in[b][:, cols], in1=pb_sb[:], op=ADD)
             residual[b] = xb
 
         natural = {}
@@ -202,6 +206,12 @@ def tile_block_pb_t_kernel(tc, attn_o, xg1, x, adj, proj_w, proj_b, gcn2_w, gcn2
             operands[b] = (vu_codes, vu_scales)
 
         graph = {}
+
+        def direct_chunks(b):
+            if b + 1 == B:
+                return (2, 3)
+            return () if b in NODIRECT else (3,)
+
         direct_sums = {}
 
         def graph_turned(b, cc):
@@ -230,7 +240,10 @@ def tile_block_pb_t_kernel(tc, attn_o, xg1, x, adj, proj_w, proj_b, gcn2_w, gcn2
 
         def graph_direct(b, cc):
             vu_codes, vu_scales = operands[b]
-            y_ps = psum_d.tile([P, Q, CHUNK], F32, tag="d", name="y_ps")
+            if len(direct_chunks(b)) == 1:
+                y_ps = psum_d.tile([P, Q, CHUNK], F32, tag="d", name="y_ps")
+            else:
+                y_ps = psum_s.tile([P, Q, CHUNK], F32, tag="s", name="y_ps")
             w_cols = slice(cc * CHUNK, (cc + 1) * CHUNK)
             for q in range(Q):
                 u_cols = slice(J + q * P, J + (q + 1) * P)
@@ -256,6 +269,9 @@ def tile_block_pb_t_kernel(tc, attn_o, xg1, x, adj, proj_w, proj_b, gcn2_w, gcn2
                 op=ADD,
             )
 
+        def turned_chunks(b):
+            return tuple(cc for cc in range(PACK) if cc not in direct_chunks(b))
+
         def begin_graph(b):
             y_grp = work.tile([P, C * PACK], BF16, tag="y_grp", name="y_grp", align_bytes=64)
             y_turned = work.tile([P, K * C * Q], BF16, tag="y_turned", name="y_turned")
@@ -265,7 +281,8 @@ def tile_block_pb_t_kernel(tc, attn_o, xg1, x, adj, proj_w, proj_b, gcn2_w, gcn2
             y_grp, y_turned = graph[b]
             words = y_turned[:].bitcast(F32)
             group_words = y_grp[:].bitcast(F32)
-            for pair in (TURNED[0:2], TURNED[2:4]):
+            turned = turned_chunks(b)
+            for pair in (turned[0:2], turned[2:4]):
                 if pair:
                     t_ps = psum_s.tile([P, len(pair) * CHUNK], F32, tag="s", name="t_ps")
                     for n, cc in enumerate(pair):
@@ -292,7 +309,10 @@ def tile_block_pb_t_kernel(tc, attn_o, xg1, x, adj, proj_w, proj_b, gcn2_w, gcn2
             y_codes, y_scales = graph[b]
             banks = []
             for q in range(Q):
-                f_ps = psum_f.tile([P, C], F32, tag="f", name="f_ps")
+                if b + 1 < B:
+                    f_ps = psum_f.tile([P, C], F32, tag="f", name="f_ps")
+                else:
+                    f_ps = psum_s.tile([P, C], F32, tag="s", name="f_ps")
                 cols = slice(q * P, (q + 1) * P)
                 nc.tensor.matmul_mx(
                     out=f_ps[:],
@@ -319,12 +339,21 @@ def tile_block_pb_t_kernel(tc, attn_o, xg1, x, adj, proj_w, proj_b, gcn2_w, gcn2
 
         def add_residual(b):
             xb = residual[b]
-            for q, width in ((1, LATE), (0, C)):
-                cols = slice(q * C, q * C + width)
-                nc.vector.tensor_tensor(out=xb[:, cols], in0=results[b][q][:, 0:width], in1=residual_in[b][:, cols], op=ADD)
-                nc.gpsimd.tensor_tensor(out=xb[:, cols], in0=xb[:, cols], in1=pb_sb[:, 0:width], op=ADD)
-            cols = slice(C + LATE, 2 * C)
-            nc.vector.tensor_tensor(out=xb[:, cols], in0=results[b][1][:, LATE:C], in1=xb[:, cols], op=ADD)
+            for q in range(Q):
+                cols = slice(q * C, (q + 1) * C)
+                late = q in late_tiles(b)
+                other = residual_in[b] if late else xb
+                nc.vector.scalar_tensor_tensor(
+                    out=xb[:, cols], in0=results[b][q][:], scalar=0.5, in1=other[:, cols], op0=MULT, op1=ADD
+                )
+
+        def add_late_bias(b, after):
+            stamp = work.tile([P, 1], F32, tag="stamp", name="stamp")
+            nc.gpsimd.tensor_copy(out=stamp[:], in_=after[:, Q * C - 1 : Q * C])
+            xb = residual[b]
+            for q in late_tiles(b):
+                cols = slice(q * C, (q + 1) * C)
+                nc.gpsimd.tensor_tensor(out=xb[:, cols], in0=xb[:, cols], in1=pb_sb[:], op=ADD)
 
         def store(b):
             xb = residual[b]
@@ -350,16 +379,12 @@ def tile_block_pb_t_kernel(tc, attn_o, xg1, x, adj, proj_w, proj_b, gcn2_w, gcn2
             chunk = wg_grp[:, cc * K * C : (cc + 1) * K * C]
             nc.vector.quantize_mx(out=wg_codes[:, cols].bitcast(FP8X4), scales=wg_scales[:, cols], in_=chunk)
 
-        wp_half = staging.tile([P, PACK * C], BF16, name="wp_half")
         wp_grp = staging.tile([P, C * PACK], BF16, name="wp_grp", align_bytes=64)
         wp_codes = consts.tile([P, C], U32, name="wp_codes", align_bytes=64)
         wp_scales = consts.tile([P, C], U8, name="wp_scales", align_bytes=64)
 
-        def halve_proj_weight():
-            nc.vector.tensor_scalar(out=wp_half[:], in0=wp_raw[:], scalar1=0.5, scalar2=None, op0=MULT)
-
         def turn_proj_weight():
-            wp_words = wp_half[:].bitcast(F32)
+            wp_words = wp_raw[:].bitcast(F32)
             for hf in range(2):
                 w_ps = psum_s.tile([P, 2, 2, P], F32, tag="s", name="wp_ps")
                 for w in range(2):
@@ -381,9 +406,12 @@ def tile_block_pb_t_kernel(tc, attn_o, xg1, x, adj, proj_w, proj_b, gcn2_w, gcn2
         def group_adjacency():
             adj_view = adj_raw[:].rearrange("p (k q mw wh) -> p wh mw k q", k=K, q=Q, wh=Q)
             for wh in range(Q):
-                nc.vector.tensor_copy(
+                nc.vector.tensor_scalar(
                     out=adj_grp[:, wh * C : (wh + 1) * C].rearrange("p (mw k q) -> p mw k q", k=K, q=Q),
-                    in_=adj_view[:, wh],
+                    in0=adj_view[:, wh],
+                    scalar1=2.0,
+                    scalar2=None,
+                    op0=MULT,
                 )
 
         def quantise_adjacency():
@@ -406,60 +434,69 @@ def tile_block_pb_t_kernel(tc, attn_o, xg1, x, adj, proj_w, proj_b, gcn2_w, gcn2
         quantise_gcn_weight(3)
 
         begin_graph(0)
-        for cc in TURNED:
+        for cc in turned_chunks(0):
             graph_turned(0, cc)
-        for cc in DIRECT:
+        for cc in direct_chunks(0):
             graph_direct(0, cc)
         fuse_streams(1)
-        for cc in DIRECT:
+        for cc in direct_chunks(0):
             add_direct_bias(0, cc)
         turn_streams(1)
         turn_graph(0)
-        double_attention(2)
-        halve_proj_weight()
-        quantise_streams(1)
-        fuse_streams(2)
         group_adjacency()
         turn_proj_weight()
-        turn_streams(2)
+        quantise_streams(1)
+        double_attention(2)
         quantise_adjacency()
+        fuse_streams(2)
         quantise_proj_weight()
-        double_attention(3)
-        fuse_streams(3)
-        turn_streams(3)
+        turn_streams(2)
 
-        for b in range(1, B + 1):
+        for b in range(1, B - 1):
             if b + AHEAD < B:
                 load_streams(b + AHEAD)
                 load_residual(b + AHEAD)
-            if b < B:
-                begin_graph(b)
-            if b < B:
-                for cc in TURNED:
-                    graph_turned(b, cc)
-            if b + 3 < B:
-                double_attention(b + 3)
-            if True:
-                quantise_graph(b - 1)
-            if b + 1 < B:
-                quantise_streams(b + 1)
-            if True:
-                output_sums(b - 1)
-            if b < B:
-                for cc in DIRECT:
-                    graph_direct(b, cc)
-            if b + 3 < B:
-                fuse_streams(b + 3)
-            if True:
-                add_proj_bias(b - 1)
-            if True:
-                add_residual(b - 1)
-            if True:
-                store(b - 1)
-            if b < B:
-                for cc in DIRECT:
-                    add_direct_bias(b, cc)
-            if b < B:
-                turn_graph(b)
-            if b + 3 < B:
-                turn_streams(b + 3)
+            begin_graph(b)
+            for cc in turned_chunks(b):
+                graph_turned(b, cc)
+            if b + 2 < B:
+                double_attention(b + 2)
+            quantise_graph(b - 1)
+            quantise_streams(b + 1)
+            output_sums(b - 1)
+            for cc in direct_chunks(b):
+                graph_direct(b, cc)
+            if b + 2 < B:
+                fuse_streams(b + 2)
+            add_proj_bias(b - 1)
+            if b > 1:
+                add_late_bias(b - 2, residual[b - 1])
+                store(b - 2)
+            add_residual(b - 1)
+            for cc in direct_chunks(b):
+                add_direct_bias(b, cc)
+            turn_graph(b)
+            if b + 2 < B:
+                turn_streams(b + 2)
+
+        b = B - 1
+        begin_graph(b)
+        for cc in turned_chunks(b):
+            graph_turned(b, cc)
+        for cc in direct_chunks(b):
+            graph_direct(b, cc)
+        quantise_graph(b - 1)
+        output_sums(b - 1)
+        add_late_bias(b - 2, residual[b - 2])
+        store(b - 2)
+        for cc in direct_chunks(b):
+            add_direct_bias(b, cc)
+        turn_graph(b)
+        add_proj_bias(b - 1)
+        quantise_graph(b)
+        output_sums(b)
+        add_residual(b - 1)
+        store(b - 1)
+        add_proj_bias(b)
+        add_residual(b)
+        store(b)

@@ -21,9 +21,8 @@ PACK = 4
 Q = J // P
 AHEAD = 6
 CHUNK = K * P
-DIRECT = (2, 3)
-
-NODIRECT = ()
+BLOCKS = K * C // P
+DIRECT = 6
 
 FLOPS = 2 * B * J * C * (C + K * C) + 2 * B * J * (K * J) * C
 
@@ -79,27 +78,36 @@ def tile_block_pb_t_kernel(tc, attn_o, xg1, x, adj, proj_w, proj_b, gcn2_w, gcn2
             nc.sync.dma_start(out=x_sb[:], in_=x[b].rearrange("(p q) c -> p (q c)", q=Q))
             residual_in[b] = x_sb
 
-        load_streams(0)
-        for cc in range(PACK):
-            load_gcn_weight_chunk(cc)
-        load_streams(1)
         adj_raw = staging.tile([P, K * Q * J], BF16, name="adj_raw")
+        wp_raw = staging.tile([P, PACK * C], BF16, name="wp_raw")
+        load_streams(0)
+        load_gcn_weight_chunk(0)
+        load_gcn_weight_chunk(1)
+        load_gcn_weight_chunk(2)
+        load_gcn_weight_chunk(3)
+        load_streams(1)
+        load_streams(2)
         nc.sync.dma_start(
             out=adj_raw[:].rearrange("p (k r) -> p k r", k=K), in_=adj.rearrange("k (m jh) w -> m k (jh w)", jh=Q)
         )
-        wp_raw = staging.tile([P, PACK * C], BF16, name="wp_raw")
         nc.sync.dma_start(
             out=wp_raw[:].rearrange("p (ot c) -> p ot c", ot=PACK), in_=proj_w.rearrange("(ot p) c -> p ot c", p=P)
         )
-        load_streams(2)
-        for b in range(AHEAD + 1):
-            load_residual(b)
-            if b + 3 <= AHEAD:
-                load_streams(b + 3)
+        load_streams(3)
+        load_streams(4)
+        load_residual(0)
+        load_residual(1)
+        load_streams(5)
+        load_residual(2)
+        load_streams(6)
+        load_residual(3)
+        load_residual(4)
+        load_residual(5)
+        load_residual(6)
 
         bias_pairs = consts.tile([P, K * C], BF16, name="bias_pairs")
         bias_col = consts.tile([P, K * PACK], F32, name="bias_col")
-        gb_sb = consts.tile([P, len(DIRECT) * CHUNK], F32, name="gb_sb")
+        gb_sb = consts.tile([P, DIRECT * P], F32, name="gb_sb")
         pb_sb = consts.tile([P, C], F32, name="pb_sb")
 
         def spread_biases():
@@ -116,12 +124,13 @@ def tile_block_pb_t_kernel(tc, attn_o, xg1, x, adj, proj_w, proj_b, gcn2_w, gcn2
                     c_ps[:, ob, :], lhsT=bias_pairs[:, ob * P : (ob + 1) * P], rhs=ones[:, 0:2], start=True, stop=True
                 )
             nc.scalar.copy(out=bias_col[:].unsqueeze(2), in_=c_ps[:, :, 0:1])
-            for n, cc in enumerate(DIRECT):
-                g_ps = psum_s.tile([P, CHUNK], F32, tag="s", name="g_ps")
-                nc.tensor.matmul(
-                    g_ps[:], lhsT=ones[:], rhs=bias_pairs[:, cc * CHUNK : (cc + 1) * CHUNK], start=True, stop=True
-                )
-                nc.scalar.copy(out=gb_sb[:, n * CHUNK : (n + 1) * CHUNK], in_=g_ps[:])
+            for first in range(BLOCKS - DIRECT, BLOCKS, DIRECT // 2):
+                width = DIRECT // 2 * P
+                g_ps = psum_s.tile([P, width], F32, tag="s", name="g_ps")
+                rhs = bias_pairs[:, first * P : first * P + width]
+                nc.tensor.matmul(g_ps[:], lhsT=ones[:], rhs=rhs, start=True, stop=True)
+                col = (first - (BLOCKS - DIRECT)) * P
+                nc.scalar.copy(out=gb_sb[:, col : col + width], in_=g_ps[:])
 
         residual = {}
 
@@ -207,70 +216,70 @@ def tile_block_pb_t_kernel(tc, attn_o, xg1, x, adj, proj_w, proj_b, gcn2_w, gcn2
 
         graph = {}
 
-        def direct_chunks(b):
-            if b + 1 == B:
-                return (2, 3)
-            return () if b in NODIRECT else (3,)
+        def direct_blocks(b):
+            return 4 if b + 1 == B else (1 if b % 2 == 0 else 2)
 
         direct_sums = {}
 
-        def graph_turned(b, cc):
+        def graph_turned(b, start, stop):
             vu_codes, vu_scales = operands[b]
             y_turned = graph[b][1]
-            y_ps = psum_s.tile([P, K, J], F32, tag="s", name="y_ps")
-            for n in range(K):
-                ob = cc * K + n
-                nc.tensor.matmul_mx(
-                    out=y_ps[:, n, :],
-                    lhsT=wg_codes[:, ob * P : (ob + 1) * P].bitcast(FP8X4),
-                    lhsT_scale=wg_scales[:, ob * P : (ob + 1) * P],
-                    rhs=vu_codes[:, J : 2 * J].bitcast(FP8X4),
-                    rhs_scale=vu_scales[:, J : 2 * J],
-                    start=True,
-                    stop=True,
-                )
-            for n in range(K):
-                ob = cc * K + n
-                nc.scalar.activation(
-                    out=y_turned[:, ob * J : (ob + 1) * J].rearrange("p (m q) -> p m q", q=Q),
-                    in_=y_ps[:, n, :].rearrange("p (q m) -> p m q", q=Q),
-                    func=IDENTITY,
-                    bias=bias_col[:, ob : ob + 1],
-                )
+            stop = min(stop, BLOCKS - direct_blocks(b))
+            for first in range(start, stop, 2):
+                blocks = range(first, min(first + 2, stop))
+                y_ps = psum_s.tile([P, 2, J], F32, tag="s", name="y_ps")
+                for ob in blocks:
+                    nc.tensor.matmul_mx(
+                        out=y_ps[:, ob - first, :],
+                        lhsT=wg_codes[:, ob * P : (ob + 1) * P].bitcast(FP8X4),
+                        lhsT_scale=wg_scales[:, ob * P : (ob + 1) * P],
+                        rhs=vu_codes[:, J : 2 * J].bitcast(FP8X4),
+                        rhs_scale=vu_scales[:, J : 2 * J],
+                        start=True,
+                        stop=True,
+                    )
+                for ob in blocks:
+                    nc.scalar.activation(
+                        out=y_turned[:, ob * J : (ob + 1) * J].rearrange("p (m q) -> p m q", q=Q),
+                        in_=y_ps[:, ob - first, :].rearrange("p (q m) -> p m q", q=Q),
+                        func=IDENTITY,
+                        bias=bias_col[:, ob : ob + 1],
+                    )
 
-        def graph_direct(b, cc):
+        def graph_direct(b):
             vu_codes, vu_scales = operands[b]
-            if len(direct_chunks(b)) == 1:
-                y_ps = psum_d.tile([P, Q, CHUNK], F32, tag="d", name="y_ps")
-            else:
-                y_ps = psum_s.tile([P, Q, CHUNK], F32, tag="s", name="y_ps")
-            w_cols = slice(cc * CHUNK, (cc + 1) * CHUNK)
-            for q in range(Q):
-                u_cols = slice(J + q * P, J + (q + 1) * P)
-                nc.tensor.matmul_mx(
-                    out=y_ps[:, q, :],
-                    lhsT=vu_codes[:, u_cols].bitcast(FP8X4),
-                    lhsT_scale=vu_scales[:, u_cols],
-                    rhs=wg_codes[:, w_cols].bitcast(FP8X4),
-                    rhs_scale=wg_scales[:, w_cols],
-                    start=True,
-                    stop=True,
-                )
-            direct_sums[b, cc] = y_ps
+            sums_of_b = []
+            for first in range(BLOCKS - direct_blocks(b), BLOCKS, 2):
+                width = min(2, BLOCKS - first) * P
+                if b + 1 < B:
+                    y_ps = psum_d.tile([P, Q, width], F32, tag="d", name="y_ps")
+                else:
+                    y_ps = psum_s.tile([P, Q, width], F32, tag="s", name="y_ps")
+                w_cols = slice(first * P, first * P + width)
+                for q in range(Q):
+                    u_cols = slice(J + q * P, J + (q + 1) * P)
+                    nc.tensor.matmul_mx(
+                        out=y_ps[:, q, :],
+                        lhsT=vu_codes[:, u_cols].bitcast(FP8X4),
+                        lhsT_scale=vu_scales[:, u_cols],
+                        rhs=wg_codes[:, w_cols].bitcast(FP8X4),
+                        rhs_scale=wg_scales[:, w_cols],
+                        start=True,
+                        stop=True,
+                    )
+                sums_of_b.append((first, width, y_ps))
+            direct_sums[b] = sums_of_b
 
-        def add_direct_bias(b, cc):
+        def add_direct_bias(b):
             y_grp = graph[b][0]
-            y_ps = direct_sums[b, cc]
-            n = DIRECT.index(cc)
-            nc.vector.tensor_tensor(
-                out=y_grp[:, cc * Q * CHUNK : (cc + 1) * Q * CHUNK].rearrange("p (o q) -> p o q", q=Q),
-                in0=y_ps[:].rearrange("p q o -> p o q"),
-                in1=gb_sb[:, n * CHUNK : (n + 1) * CHUNK].unsqueeze(2).to_broadcast([P, CHUNK, Q]),
-                op=ADD,
-            )
-
-        def turned_chunks(b):
-            return tuple(cc for cc in range(PACK) if cc not in direct_chunks(b))
+            for first, width, y_ps in direct_sums[b]:
+                col = (first - (BLOCKS - DIRECT)) * P
+                nc.vector.tensor_tensor(
+                    out=y_grp[:, first * P * Q : (first * P + width) * Q].rearrange("p (o q) -> p o q", q=Q),
+                    in0=y_ps[:].rearrange("p q o -> p o q"),
+                    in1=gb_sb[:, col : col + width].unsqueeze(2).to_broadcast([P, width, Q]),
+                    op=ADD,
+                )
 
         def begin_graph(b):
             y_grp = work.tile([P, C * PACK], BF16, tag="y_grp", name="y_grp", align_bytes=64)
@@ -281,20 +290,14 @@ def tile_block_pb_t_kernel(tc, attn_o, xg1, x, adj, proj_w, proj_b, gcn2_w, gcn2
             y_grp, y_turned = graph[b]
             words = y_turned[:].bitcast(F32)
             group_words = y_grp[:].bitcast(F32)
-            turned = turned_chunks(b)
-            for pair in (turned[0:2], turned[2:4]):
-                if pair:
-                    t_ps = psum_s.tile([P, len(pair) * CHUNK], F32, tag="s", name="t_ps")
-                    for n, cc in enumerate(pair):
-                        for half in range(K):
-                            col = cc * CHUNK + half * P
-                            nc.tensor.transpose(
-                                t_ps[:, n * CHUNK + half * P : n * CHUNK + (half + 1) * P],
-                                words[:, col : col + P],
-                                ident_f32[:],
-                            )
-                    first = pair[0] * CHUNK
-                    nc.scalar.copy(out=group_words[:, first : first + len(pair) * CHUNK], in_=t_ps[:])
+            turned = BLOCKS - direct_blocks(b)
+            for first in range(0, turned, 4):
+                width = min(4, turned - first) * P
+                t_ps = psum_s.tile([P, width], F32, tag="s", name="t_ps")
+                for col in range(0, width, P):
+                    at = first * P + col
+                    nc.tensor.transpose(t_ps[:, col : col + P], words[:, at : at + P], ident_f32[:])
+                nc.scalar.copy(out=group_words[:, first * P : first * P + width], in_=t_ps[:])
 
         def quantise_graph(b):
             y_codes = work.tile([P, C], U32, tag="y_codes", name="y_codes", align_bytes=64)
@@ -348,7 +351,7 @@ def tile_block_pb_t_kernel(tc, attn_o, xg1, x, adj, proj_w, proj_b, gcn2_w, gcn2
                 )
 
         def add_late_bias(b, after):
-            stamp = work.tile([P, 1], F32, tag="stamp", name="stamp")
+            stamp = work.tile([P, 1], BF16, tag="stamp", name="stamp")
             nc.gpsimd.tensor_copy(out=stamp[:], in_=after[:, Q * C - 1 : Q * C])
             xb = residual[b]
             for q in late_tiles(b):
@@ -421,78 +424,85 @@ def tile_block_pb_t_kernel(tc, attn_o, xg1, x, adj, proj_w, proj_b, gcn2_w, gcn2
         spread_biases()
         double_attention(0)
         fuse_streams(0)
-        turn_streams(0)
         turn_gcn_weight(0, nc.vector.tensor_copy)
+        turn_streams(0)
         turn_gcn_weight(1, nc.scalar.copy)
-        quantise_streams(0)
         quantise_gcn_weight(0)
         turn_gcn_weight(2, nc.vector.tensor_copy)
+        quantise_streams(0)
         quantise_gcn_weight(1)
         turn_gcn_weight(3, nc.scalar.copy)
         double_attention(1)
         quantise_gcn_weight(2)
-        quantise_gcn_weight(3)
-
-        begin_graph(0)
-        for cc in turned_chunks(0):
-            graph_turned(0, cc)
-        for cc in direct_chunks(0):
-            graph_direct(0, cc)
         fuse_streams(1)
-        for cc in direct_chunks(0):
-            add_direct_bias(0, cc)
+        quantise_gcn_weight(3)
+        begin_graph(0)
+        graph_turned(0, 0, 4)
         turn_streams(1)
-        turn_graph(0)
+        graph_turned(0, 4, BLOCKS)
+        graph_direct(0)
+        double_attention(2)
+        fuse_streams(2)
+        quantise_streams(1)
         group_adjacency()
         turn_proj_weight()
-        quantise_streams(1)
-        double_attention(2)
         quantise_adjacency()
-        fuse_streams(2)
         quantise_proj_weight()
-        turn_streams(2)
 
-        for b in range(1, B - 1):
-            if b + AHEAD < B:
-                load_streams(b + AHEAD)
-                load_residual(b + AHEAD)
-            begin_graph(b)
-            for cc in turned_chunks(b):
-                graph_turned(b, cc)
-            if b + 2 < B:
-                double_attention(b + 2)
-            quantise_graph(b - 1)
-            quantise_streams(b + 1)
-            output_sums(b - 1)
-            for cc in direct_chunks(b):
-                graph_direct(b, cc)
-            if b + 2 < B:
-                fuse_streams(b + 2)
-            add_proj_bias(b - 1)
-            if b > 1:
-                add_late_bias(b - 2, residual[b - 1])
-                store(b - 2)
-            add_residual(b - 1)
-            for cc in direct_chunks(b):
-                add_direct_bias(b, cc)
-            turn_graph(b)
-            if b + 2 < B:
+        for b in range(0, B - 1):
+            if 7 <= b + 6 < B:
+                load_streams(b + 6)
+            if 7 <= b + 6 < B:
+                load_residual(b + 6)
+            if 0 <= b - 3 < B - 2:
+                add_late_bias(b - 3, natural[min(b + 2, B - 1)][3])
+            if 0 <= b - 1 < B:
+                add_direct_bias(b - 1)
+            if 0 <= b - 2 < B:
+                add_residual(b - 2)
+            if 3 <= b + 3 < B:
+                double_attention(b + 3)
+            if 2 <= b + 1 < B:
+                quantise_streams(b + 1)
+            if 0 <= b - 1 < B:
+                turn_graph(b - 1)
+            if 2 <= b + 2 < B:
                 turn_streams(b + 2)
+            if 1 <= b < B:
+                begin_graph(b)
+            if 1 <= b < B:
+                graph_turned(b, 0, 4)
+            if 0 <= b - 1 < B:
+                quantise_graph(b - 1)
+            if 1 <= b < B:
+                graph_direct(b)
+            if 1 <= b < B:
+                graph_turned(b, 4, BLOCKS)
+            if 0 <= b - 1 < B:
+                output_sums(b - 1)
+            if 0 <= b - 1 < B:
+                add_proj_bias(b - 1)
+            if 3 <= b + 3 < B:
+                fuse_streams(b + 3)
+            if 0 <= b - 3 < B:
+                store(b - 3)
 
         b = B - 1
         begin_graph(b)
-        for cc in turned_chunks(b):
-            graph_turned(b, cc)
-        for cc in direct_chunks(b):
-            graph_direct(b, cc)
+        turn_graph(b - 1)
+        graph_turned(b, 0, BLOCKS)
+        graph_direct(b)
+        add_late_bias(b - 3, natural[b][3])
+        store(b - 3)
+        add_residual(b - 2)
+        add_direct_bias(b - 1)
         quantise_graph(b - 1)
         output_sums(b - 1)
-        add_late_bias(b - 2, residual[b - 2])
-        store(b - 2)
-        for cc in direct_chunks(b):
-            add_direct_bias(b, cc)
         turn_graph(b)
         add_proj_bias(b - 1)
+        add_late_bias(b - 2, natural[b][3])
+        store(b - 2)
+        add_direct_bias(b)
         quantise_graph(b)
         output_sums(b)
         add_residual(b - 1)

@@ -22,7 +22,7 @@ Q = J // P
 AHEAD = 6
 CHUNK = K * P
 BLOCKS = K * C // P
-DIRECT = 6
+DIRECT = 2
 
 FLOPS = 2 * B * J * C * (C + K * C) + 2 * B * J * (K * J) * C
 
@@ -34,7 +34,7 @@ def tile_block_pb_t_kernel(tc, attn_o, xg1, x, adj, proj_w, proj_b, gcn2_w, gcn2
         staging = stack.enter_context(tc.tile_pool(name="staging", bufs=1))
         loads = stack.enter_context(tc.tile_pool(name="loads", bufs=8))
         sums = stack.enter_context(tc.tile_pool(name="sums", bufs=8))
-        work = stack.enter_context(tc.tile_pool(name="work", bufs=3))
+        work = stack.enter_context(tc.tile_pool(name="work", bufs=4))
         psum_s = stack.enter_context(tc.psum_pool(name="psum_s", bufs=5))
         psum_d = stack.enter_context(tc.psum_pool(name="psum_d", bufs=1))
         psum_f = stack.enter_context(tc.psum_pool(name="psum_f", bufs=2))
@@ -124,13 +124,9 @@ def tile_block_pb_t_kernel(tc, attn_o, xg1, x, adj, proj_w, proj_b, gcn2_w, gcn2
                     c_ps[:, ob, :], lhsT=bias_pairs[:, ob * P : (ob + 1) * P], rhs=ones[:, 0:2], start=True, stop=True
                 )
             nc.scalar.copy(out=bias_col[:].unsqueeze(2), in_=c_ps[:, :, 0:1])
-            for first in range(BLOCKS - DIRECT, BLOCKS, DIRECT // 2):
-                width = DIRECT // 2 * P
-                g_ps = psum_s.tile([P, width], F32, tag="s", name="g_ps")
-                rhs = bias_pairs[:, first * P : first * P + width]
-                nc.tensor.matmul(g_ps[:], lhsT=ones[:], rhs=rhs, start=True, stop=True)
-                col = (first - (BLOCKS - DIRECT)) * P
-                nc.scalar.copy(out=gb_sb[:, col : col + width], in_=g_ps[:])
+            g_ps = psum_s.tile([P, DIRECT * P], F32, tag="s", name="g_ps")
+            nc.tensor.matmul(g_ps[:], lhsT=ones[:], rhs=bias_pairs[:, (BLOCKS - DIRECT) * P :], start=True, stop=True)
+            nc.scalar.copy(out=gb_sb[:], in_=g_ps[:])
 
         residual = {}
 
@@ -217,7 +213,7 @@ def tile_block_pb_t_kernel(tc, attn_o, xg1, x, adj, proj_w, proj_b, gcn2_w, gcn2
         graph = {}
 
         def direct_blocks(b):
-            return 4 if b + 1 == B else (1 if b % 2 == 0 else 2)
+            return 1 if b % 2 == 0 else 2
 
         direct_sums = {}
 
@@ -251,10 +247,7 @@ def tile_block_pb_t_kernel(tc, attn_o, xg1, x, adj, proj_w, proj_b, gcn2_w, gcn2
             sums_of_b = []
             for first in range(BLOCKS - direct_blocks(b), BLOCKS, 2):
                 width = min(2, BLOCKS - first) * P
-                if b + 1 < B:
-                    y_ps = psum_d.tile([P, Q, width], F32, tag="d", name="y_ps")
-                else:
-                    y_ps = psum_s.tile([P, Q, width], F32, tag="s", name="y_ps")
+                y_ps = psum_d.tile([P, Q, width], F32, tag="d", name="y_ps")
                 w_cols = slice(first * P, first * P + width)
                 for q in range(Q):
                     u_cols = slice(J + q * P, J + (q + 1) * P)
@@ -312,10 +305,7 @@ def tile_block_pb_t_kernel(tc, attn_o, xg1, x, adj, proj_w, proj_b, gcn2_w, gcn2
             y_codes, y_scales = graph[b]
             banks = []
             for q in range(Q):
-                if b + 1 < B:
-                    f_ps = psum_f.tile([P, C], F32, tag="f", name="f_ps")
-                else:
-                    f_ps = psum_s.tile([P, C], F32, tag="s", name="f_ps")
+                f_ps = psum_f.tile([P, C], F32, tag="f", name="f_ps")
                 cols = slice(q * P, (q + 1) * P)
                 nc.tensor.matmul_mx(
                     out=f_ps[:],
@@ -444,69 +434,49 @@ def tile_block_pb_t_kernel(tc, attn_o, xg1, x, adj, proj_w, proj_b, gcn2_w, gcn2
         double_attention(2)
         fuse_streams(2)
         quantise_streams(1)
+        add_direct_bias(0)
+        turn_graph(0)
         group_adjacency()
         turn_proj_weight()
         quantise_adjacency()
-        quantise_proj_weight()
 
-        for b in range(0, B - 1):
+        for b in range(0, B + 4):
             if 7 <= b + 6 < B:
                 load_streams(b + 6)
             if 7 <= b + 6 < B:
                 load_residual(b + 6)
-            if 0 <= b - 3 < B - 2:
-                add_late_bias(b - 3, natural[min(b + 2, B - 1)][3])
-            if 0 <= b - 1 < B:
+            if 0 <= b - 4 < B - 2:
+                add_late_bias(b - 4, natural[min(b + 2, B - 1)][3])
+            if 0 <= b - 3 < B:
+                add_residual(b - 3)
+            if 1 <= b - 1 < B:
                 add_direct_bias(b - 1)
-            if 0 <= b - 2 < B:
-                add_residual(b - 2)
             if 3 <= b + 3 < B:
                 double_attention(b + 3)
             if 2 <= b + 1 < B:
                 quantise_streams(b + 1)
-            if 0 <= b - 1 < B:
-                turn_graph(b - 1)
             if 2 <= b + 2 < B:
                 turn_streams(b + 2)
+            if 1 <= b - 1 < B:
+                turn_graph(b - 1)
             if 1 <= b < B:
                 begin_graph(b)
             if 1 <= b < B:
                 graph_turned(b, 0, 4)
-            if 0 <= b - 1 < B:
-                quantise_graph(b - 1)
             if 1 <= b < B:
                 graph_direct(b)
             if 1 <= b < B:
                 graph_turned(b, 4, BLOCKS)
-            if 0 <= b - 1 < B:
-                output_sums(b - 1)
-            if 0 <= b - 1 < B:
-                add_proj_bias(b - 1)
+            if 0 <= b - 2 < B:
+                output_sums(b - 2)
             if 3 <= b + 3 < B:
                 fuse_streams(b + 3)
-            if 0 <= b - 3 < B:
-                store(b - 3)
-
-        b = B - 1
-        begin_graph(b)
-        turn_graph(b - 1)
-        graph_turned(b, 0, BLOCKS)
-        graph_direct(b)
-        add_late_bias(b - 3, natural[b][3])
-        store(b - 3)
-        add_residual(b - 2)
-        add_direct_bias(b - 1)
-        quantise_graph(b - 1)
-        output_sums(b - 1)
-        turn_graph(b)
-        add_proj_bias(b - 1)
-        add_late_bias(b - 2, natural[b][3])
-        store(b - 2)
-        add_direct_bias(b)
-        quantise_graph(b)
-        output_sums(b)
-        add_residual(b - 1)
-        store(b - 1)
-        add_proj_bias(b)
-        add_residual(b)
-        store(b)
+            if 0 <= b - 2 < B:
+                add_proj_bias(b - 2)
+            if 1 <= b - 1 < B:
+                quantise_graph(b - 1)
+            if 0 <= b - 4 < B:
+                store(b - 4)
+            if b == 0:
+                quantise_proj_weight()
+                quantise_graph(0)

from contextlib import ExitStack

import concourse.mybir as mybir
from concourse.masks import make_identity

FP8X4 = mybir.dt.float8_e4m3fn_x4
BF16 = mybir.dt.bfloat16
F32 = mybir.dt.float32
U32 = mybir.dt.uint32
U8 = mybir.dt.uint8
ADD = mybir.AluOpType.add
MULT = mybir.AluOpType.mult
COPY = mybir.ActivationFunctionType.Copy
ENGINES = mybir.EngineType
IDENTITY = mybir.ActivationFunctionType.Identity

B, J, C, K, H = 16, 256, 512, 2, 8
DH = C // H
P = 128
PACK = 4
Q = J // P
AHEAD = 6
CHUNK = K * P
BLOCKS = K * C // P
DIRECT = 2

FLOPS = 2 * B * J * C * (C + K * C) + 2 * B * J * (K * J) * C


def tile_block_pb_t_kernel(tc, attn_o, xg1, x, adj, proj_w, proj_b, gcn2_w, gcn2_b, out):
    nc = tc.nc
    with ExitStack() as stack:
        consts = stack.enter_context(tc.tile_pool(name="consts", bufs=1))
        staging = stack.enter_context(tc.tile_pool(name="staging", bufs=1))
        loads = stack.enter_context(tc.tile_pool(name="loads", bufs=8))
        sums = stack.enter_context(tc.tile_pool(name="sums", bufs=8))
        work = stack.enter_context(tc.tile_pool(name="work", bufs=4))
        psum_s = stack.enter_context(tc.psum_pool(name="psum_s", bufs=5))
        psum_d = stack.enter_context(tc.psum_pool(name="psum_d", bufs=1))
        psum_f = stack.enter_context(tc.psum_pool(name="psum_f", bufs=2))

        bias_row = consts.tile([P, K * C + C], BF16, name="bias_row")
        nc.vector.memset(bias_row[:], 0.0)
        nc.scalar.dma_start(out=bias_row[0:1, 0 : K * C], in_=gcn2_b.unsqueeze(0))
        nc.scalar.dma_start(out=bias_row[0:1, K * C : K * C + C], in_=proj_b.unsqueeze(0))
        ident_f32 = consts.tile([P, P], F32, name="ident_f32")
        make_identity(nc, ident_f32[:])
        ident_bf = consts.tile([P, P], BF16, name="ident_bf")
        make_identity(nc, ident_bf[:])
        ident_25 = consts.tile([P, P], BF16, name="ident_25")
        nc.vector.tensor_scalar(out=ident_25[:], in0=ident_bf[:], scalar1=2.5, scalar2=None, op0=MULT)
        ones = consts.tile([P, P], BF16, name="ones")
        nc.vector.memset(ones[:], 1.0)

        wg_raw = staging.tile([P, PACK * K * C], BF16, name="wg_raw")
        wg_rows = gcn2_w.rearrange("(k cc p) c -> cc p k c", k=K, cc=PACK)

        def load_gcn_weight_chunk(cc):
            nc.sync.dma_start(
                out=wg_raw[:, cc * K * C : (cc + 1) * K * C].rearrange("p (k c) -> p k c", k=K), in_=wg_rows[cc]
            )

        streams = {}

        def load_streams(b):
            a_raw = loads.tile([P, Q * C], BF16, tag="a_raw", name="a_raw")
            nc.sync.dma_start(
                out=a_raw[:].rearrange("p (h r) -> p h r", h=H), in_=attn_o[b].rearrange("h (p q) d -> p h (q d)", q=Q)
            )
            g_raw = loads.tile([P, Q * C], BF16, tag="g_raw", name="g_raw")
            nc.sync.dma_start(out=g_raw[:], in_=xg1[b].rearrange("(p q) c -> p (q c)", q=Q))
            streams[b] = (a_raw, g_raw)

        residual_in = {}

        def load_residual(b):
            x_sb = loads.tile([P, Q * C], BF16, tag="x_sb", name="x_sb")
            nc.sync.dma_start(out=x_sb[:], in_=x[b].rearrange("(p q) c -> p (q c)", q=Q))
            residual_in[b] = x_sb

        adj_raw = staging.tile([P, K * Q * J], BF16, name="adj_raw")
        wp_raw = staging.tile([P, PACK * C], BF16, name="wp_raw")
        load_streams(0)
        load_gcn_weight_chunk(0)
        load_gcn_weight_chunk(1)
        load_gcn_weight_chunk(2)
        load_gcn_weight_chunk(3)
        load_streams(1)
        load_streams(2)
        nc.sync.dma_start(
            out=adj_raw[:].rearrange("p (k r) -> p k r", k=K), in_=adj.rearrange("k (m jh) w -> m k (jh w)", jh=Q)
        )
        nc.sync.dma_start(
            out=wp_raw[:].rearrange("p (ot c) -> p ot c", ot=PACK), in_=proj_w.rearrange("(ot p) c -> p ot c", p=P)
        )
        load_streams(3)
        load_streams(4)
        load_residual(0)
        load_residual(1)
        load_streams(5)
        load_residual(2)
        load_streams(6)
        load_residual(3)
        load_residual(4)
        load_residual(5)
        load_residual(6)

        bias_pairs = consts.tile([P, K * C], BF16, name="bias_pairs")
        bias_col = consts.tile([P, K * PACK], F32, name="bias_col")
        gb_sb = consts.tile([P, DIRECT * P], F32, name="gb_sb")
        pb_sb = consts.tile([P, C], F32, name="pb_sb")

        def spread_biases():
            nc.vector.tensor_copy(
                out=bias_pairs[:].rearrange("p (c k) -> p c k", k=K),
                in_=bias_row[:, 0 : K * C].rearrange("p (k c) -> p c k", k=K),
            )
            p_ps = psum_s.tile([P, C], F32, tag="s", name="p_ps")
            nc.tensor.matmul(p_ps[:], lhsT=ones[:], rhs=bias_row[:, K * C : K * C + C], start=True, stop=True)
            nc.scalar.copy(out=pb_sb[:], in_=p_ps[:])
            c_ps = psum_s.tile([P, K * PACK, 2], F32, tag="s", name="c_ps")
            for ob in range(K * PACK):
                nc.tensor.matmul(
                    c_ps[:, ob, :], lhsT=bias_pairs[:, ob * P : (ob + 1) * P], rhs=ones[:, 0:2], start=True, stop=True
                )
            nc.scalar.copy(out=bias_col[:].unsqueeze(2), in_=c_ps[:, :, 0:1])
            g_ps = psum_s.tile([P, DIRECT * P], F32, tag="s", name="g_ps")
            nc.tensor.matmul(g_ps[:], lhsT=ones[:], rhs=bias_pairs[:, (BLOCKS - DIRECT) * P :], start=True, stop=True)
            nc.scalar.copy(out=gb_sb[:], in_=g_ps[:])

        residual = {}

        def late_tiles(b):
            return (0,) if b + 2 < B else ()

        def add_proj_bias(b):
            xb = sums.tile([P, Q * C], F32, tag="xb", name="xb")
            for q in range(Q):
                if q not in late_tiles(b):
                    cols = slice(q * C, (q + 1) * C)
                    nc.vector.tensor_tensor(out=xb[:, cols], in0=residual_in[b][:, cols], in1=pb_sb[:], op=ADD)
            residual[b] = xb

        natural = {}

        def plain_tiles(b):
            return (0, 1) if b % 2 else (0,)

        def double_attention(b):
            a_raw, g_raw = streams[b]
            a2 = work.tile([P, Q * C], BF16, tag="a2", name="a2")
            nc.vector.tensor_scalar(
                out=a2[:].rearrange("p (q h d) -> p q h d", q=Q, h=H),
                in0=a_raw[:].rearrange("p (h q d) -> p q h d", h=H, q=Q),
                scalar1=2.0,
                scalar2=None,
                op0=MULT,
            )
            natural[b] = (a2, g_raw)

        def fuse_streams(b):
            a2, g_raw = natural[b]
            v_nat = work.tile([P, Q * C], BF16, tag="v_nat", name="v_nat")
            nc.vector.tensor_tensor(out=v_nat[:], in0=a2[:], in1=g_raw[:], op=ADD)
            u_nat = None
            if 1 not in plain_tiles(b):
                u_nat = work.tile([P, C], BF16, tag="u_nat", name="u_nat")
                nc.vector.scalar_tensor_tensor(
                    out=u_nat[:], in0=a2[:, C : 2 * C], scalar=0.4, in1=g_raw[:, C : 2 * C], op0=MULT, op1=ADD
                )
            natural[b] = (a2, g_raw, u_nat, v_nat)

        grouped = {}

        def turn_streams(b):
            a2, g_raw, u_nat, v_nat = natural[b]
            vu_grp = work.tile([P, 2 * J * PACK], BF16, tag="vu_grp", name="vu_grp", align_bytes=64)
            v_words = v_nat[:].bitcast(F32)
            v_ps = psum_s.tile([P, Q, 2, P], F32, tag="s", name="v_ps")
            for q in range(Q):
                for w in range(2):
                    col = (2 * q + w) * P
                    nc.tensor.transpose(v_ps[:, q, w, :], v_words[:, col : col + P], ident_f32[:])
            nc.scalar.copy(
                out=vu_grp[:].bitcast(F32)[:, 0 : J * 2].rearrange("p (q m w) -> p q m w", q=Q, w=2),
                in_=v_ps[:].rearrange("p q w m -> p q m w"),
            )
            for q in range(Q):
                first = (J + q * P) * PACK
                u_out = vu_grp[:, first : first + P * PACK].rearrange("p (m t) -> p m t", t=PACK)
                if q in plain_tiles(b):
                    s_ps = psum_s.tile([P, PACK, P], F32, tag="s", name="s_ps")
                    for t in range(PACK):
                        cols = slice(q * C + t * P, q * C + (t + 1) * P)
                        nc.tensor.matmul(s_ps[:, t, :], lhsT=a2[:, cols], rhs=ident_bf[:], start=True, stop=False)
                        nc.tensor.matmul(s_ps[:, t, :], lhsT=g_raw[:, cols], rhs=ident_25[:], start=False, stop=True)
                    nc.scalar.activation(out=u_out, in_=s_ps[:].rearrange("p t m -> p m t"), func=COPY, scale=0.4)
                else:
                    u_ps = psum_s.tile([P, PACK, P], BF16, tag="s", name="u_ps")
                    for t in range(PACK):
                        nc.tensor.transpose(u_ps[:, t, :], u_nat[:, t * P : (t + 1) * P], ident_bf[:])
                    nc.scalar.copy(out=u_out, in_=u_ps[:].rearrange("p t m -> p m t"))
            grouped[b] = vu_grp

        operands = {}

        def quantise_streams(b):
            vu_codes = work.tile([P, 2 * J], U32, tag="vu_codes", name="vu_codes", align_bytes=64)
            vu_scales = work.tile([P, 2 * J], U8, tag="vu_scales", name="vu_scales", align_bytes=64)
            nc.vector.quantize_mx(out=vu_codes[:].bitcast(FP8X4), scales=vu_scales[:], in_=grouped[b][:])
            operands[b] = (vu_codes, vu_scales)

        graph = {}

        def direct_blocks(b):
            return 1 if b % 2 == 0 else 2

        direct_sums = {}

        def graph_turned(b, start, stop):
            vu_codes, vu_scales = operands[b]
            y_turned = graph[b][1]
            stop = min(stop, BLOCKS - direct_blocks(b))
            for first in range(start, stop, 2):
                blocks = range(first, min(first + 2, stop))
                y_ps = psum_s.tile([P, 2, J], F32, tag="s", name="y_ps")
                for ob in blocks:
                    nc.tensor.matmul_mx(
                        out=y_ps[:, ob - first, :],
                        lhsT=wg_codes[:, ob * P : (ob + 1) * P].bitcast(FP8X4),
                        lhsT_scale=wg_scales[:, ob * P : (ob + 1) * P],
                        rhs=vu_codes[:, J : 2 * J].bitcast(FP8X4),
                        rhs_scale=vu_scales[:, J : 2 * J],
                        start=True,
                        stop=True,
                    )
                for ob in blocks:
                    nc.scalar.activation(
                        out=y_turned[:, ob * J : (ob + 1) * J].rearrange("p (m q) -> p m q", q=Q),
                        in_=y_ps[:, ob - first, :].rearrange("p (q m) -> p m q", q=Q),
                        func=IDENTITY,
                        bias=bias_col[:, ob : ob + 1],
                    )

        def graph_direct(b):
            vu_codes, vu_scales = operands[b]
            sums_of_b = []
            for first in range(BLOCKS - direct_blocks(b), BLOCKS, 2):
                width = min(2, BLOCKS - first) * P
                y_ps = psum_d.tile([P, Q, width], F32, tag="d", name="y_ps")
                w_cols = slice(first * P, first * P + width)
                for q in range(Q):
                    u_cols = slice(J + q * P, J + (q + 1) * P)
                    nc.tensor.matmul_mx(
                        out=y_ps[:, q, :],
                        lhsT=vu_codes[:, u_cols].bitcast(FP8X4),
                        lhsT_scale=vu_scales[:, u_cols],
                        rhs=wg_codes[:, w_cols].bitcast(FP8X4),
                        rhs_scale=wg_scales[:, w_cols],
                        start=True,
                        stop=True,
                    )
                sums_of_b.append((first, width, y_ps))
            direct_sums[b] = sums_of_b

        def add_direct_bias(b):
            y_grp = graph[b][0]
            for first, width, y_ps in direct_sums[b]:
                col = (first - (BLOCKS - DIRECT)) * P
                nc.vector.tensor_tensor(
                    out=y_grp[:, first * P * Q : (first * P + width) * Q].rearrange("p (o q) -> p o q", q=Q),
                    in0=y_ps[:].rearrange("p q o -> p o q"),
                    in1=gb_sb[:, col : col + width].unsqueeze(2).to_broadcast([P, width, Q]),
                    op=ADD,
                )

        def begin_graph(b):
            y_grp = work.tile([P, C * PACK], BF16, tag="y_grp", name="y_grp", align_bytes=64)
            y_turned = work.tile([P, K * C * Q], BF16, tag="y_turned", name="y_turned")
            graph[b] = (y_grp, y_turned)

        def turn_graph(b):
            y_grp, y_turned = graph[b]
            words = y_turned[:].bitcast(F32)
            group_words = y_grp[:].bitcast(F32)
            turned = BLOCKS - direct_blocks(b)
            for first in range(0, turned, 4):
                width = min(4, turned - first) * P
                t_ps = psum_s.tile([P, width], F32, tag="s", name="t_ps")
                for col in range(0, width, P):
                    at = first * P + col
                    nc.tensor.transpose(t_ps[:, col : col + P], words[:, at : at + P], ident_f32[:])
                nc.scalar.copy(out=group_words[:, first * P : first * P + width], in_=t_ps[:])

        def quantise_graph(b):
            y_codes = work.tile([P, C], U32, tag="y_codes", name="y_codes", align_bytes=64)
            y_scales = work.tile([P, C], U8, tag="y_scales", name="y_scales", align_bytes=64)
            nc.vector.quantize_mx(out=y_codes[:].bitcast(FP8X4), scales=y_scales[:], in_=graph[b][0][:])
            graph[b] = (y_codes, y_scales)

        results = {}

        def output_sums(b):
            vu_codes, vu_scales = operands[b]
            y_codes, y_scales = graph[b]
            banks = []
            for q in range(Q):
                f_ps = psum_f.tile([P, C], F32, tag="f", name="f_ps")
                cols = slice(q * P, (q + 1) * P)
                nc.tensor.matmul_mx(
                    out=f_ps[:],
                    lhsT=vu_codes[:, cols].bitcast(FP8X4),
                    lhsT_scale=vu_scales[:, cols],
                    rhs=wp_codes[:].bitcast(FP8X4),
                    rhs_scale=wp_scales[:],
                    start=True,
                    stop=False,
                )
                banks.append(f_ps)
            for q in range(Q):
                cols = slice(q * P, (q + 1) * P)
                nc.tensor.matmul_mx(
                    out=banks[q][:],
                    lhsT=adj_codes[:, cols].bitcast(FP8X4),
                    lhsT_scale=adj_scales[:, cols],
                    rhs=y_codes[:].bitcast(FP8X4),
                    rhs_scale=y_scales[:],
                    start=False,
                    stop=True,
                )
            results[b] = banks

        def add_residual(b):
            xb = residual[b]
            for q in range(Q):
                cols = slice(q * C, (q + 1) * C)
                late = q in late_tiles(b)
                other = residual_in[b] if late else xb
                nc.vector.scalar_tensor_tensor(
                    out=xb[:, cols], in0=results[b][q][:], scalar=0.5, in1=other[:, cols], op0=MULT, op1=ADD
                )

        def add_late_bias(b, after):
            stamp = work.tile([P, 1], BF16, tag="stamp", name="stamp")
            nc.gpsimd.tensor_copy(out=stamp[:], in_=after[:, Q * C - 1 : Q * C])
            xb = residual[b]
            for q in late_tiles(b):
                cols = slice(q * C, (q + 1) * C)
                nc.gpsimd.tensor_tensor(out=xb[:, cols], in0=xb[:, cols], in1=pb_sb[:], op=ADD)

        def store(b):
            xb = residual[b]
            nc.sync.dma_start(out=out[b].rearrange("(p q) c -> p (q c)", q=Q), in_=xb[:])

        wg_grp = staging.tile([P, K * C * PACK], BF16, name="wg_grp", align_bytes=64)
        wg_codes = consts.tile([P, K * C], U32, name="wg_codes", align_bytes=64)
        wg_scales = consts.tile([P, K * C], U8, name="wg_scales", align_bytes=64)

        def turn_gcn_weight(cc, copy):
            w_ps = psum_s.tile([P, PACK, K, P], BF16, tag="s", name="w_ps")
            for t in range(PACK):
                for k in range(K):
                    col = (cc * K + k) * C + t * P
                    nc.tensor.transpose(w_ps[:, t, k, :], wg_raw[:, col : col + P], ident_bf[:])
            chunk = wg_grp[:, cc * K * C : (cc + 1) * K * C]
            copy(
                out=chunk.rearrange("p (c k t) -> p c k t", k=K, t=PACK), in_=w_ps[:].rearrange("p t k c -> p c k t")
            )

        def quantise_gcn_weight(cc):
            cols = slice(cc * CHUNK, (cc + 1) * CHUNK)
            chunk = wg_grp[:, cc * K * C : (cc + 1) * K * C]
            nc.vector.quantize_mx(out=wg_codes[:, cols].bitcast(FP8X4), scales=wg_scales[:, cols], in_=chunk)

        wp_grp = staging.tile([P, C * PACK], BF16, name="wp_grp", align_bytes=64)
        wp_codes = consts.tile([P, C], U32, name="wp_codes", align_bytes=64)
        wp_scales = consts.tile([P, C], U8, name="wp_scales", align_bytes=64)

        def turn_proj_weight():
            wp_words = wp_raw[:].bitcast(F32)
            for hf in range(2):
                w_ps = psum_s.tile([P, 2, 2, P], F32, tag="s", name="wp_ps")
                for w in range(2):
                    for o2 in range(2):
                        col = (hf * 2 + o2) * (C // 2) + w * P
                        nc.tensor.transpose(w_ps[:, w, o2, :], wp_words[:, col : col + P], ident_f32[:])
                nc.scalar.copy(
                    out=wp_grp[:].bitcast(F32)[:, hf * C : (hf + 1) * C].rearrange("p (o w) -> p o w", w=2),
                    in_=w_ps[:].rearrange("p w o2 o -> p (o2 o) w"),
                )

        def quantise_proj_weight():
            nc.vector.quantize_mx(out=wp_codes[:].bitcast(FP8X4), scales=wp_scales[:], in_=wp_grp[:])

        adj_grp = staging.tile([P, J * PACK], BF16, name="adj_grp", align_bytes=64)
        adj_codes = consts.tile([P, J], U32, name="adj_codes", align_bytes=64)
        adj_scales = consts.tile([P, J], U8, name="adj_scales", align_bytes=64)

        def group_adjacency():
            adj_view = adj_raw[:].rearrange("p (k q mw wh) -> p wh mw k q", k=K, q=Q, wh=Q)
            for wh in range(Q):
                nc.vector.tensor_scalar(
                    out=adj_grp[:, wh * C : (wh + 1) * C].rearrange("p (mw k q) -> p mw k q", k=K, q=Q),
                    in0=adj_view[:, wh],
                    scalar1=2.0,
                    scalar2=None,
                    op0=MULT,
                )

        def quantise_adjacency():
            nc.vector.quantize_mx(out=adj_codes[:].bitcast(FP8X4), scales=adj_scales[:], in_=adj_grp[:])

        stack.enter_context(tc.manual_schedule(engines={ENGINES.PE, ENGINES.DVE, ENGINES.Activation, ENGINES.Pool}))
        spread_biases()
        double_attention(0)
        fuse_streams(0)
        turn_gcn_weight(0, nc.vector.tensor_copy)
        turn_streams(0)
        turn_gcn_weight(1, nc.scalar.copy)
        quantise_gcn_weight(0)
        turn_gcn_weight(2, nc.vector.tensor_copy)
        quantise_streams(0)
        quantise_gcn_weight(1)
        turn_gcn_weight(3, nc.scalar.copy)
        double_attention(1)
        quantise_gcn_weight(2)
        fuse_streams(1)
        quantise_gcn_weight(3)
        begin_graph(0)
        graph_turned(0, 0, 4)
        turn_streams(1)
        graph_turned(0, 4, BLOCKS)
        graph_direct(0)
        double_attention(2)
        fuse_streams(2)
        quantise_streams(1)
        add_direct_bias(0)
        turn_graph(0)
        group_adjacency()
        turn_proj_weight()
        quantise_adjacency()

        for b in range(0, B + 4):
            if 7 <= b + 6 < B:
                load_streams(b + 6)
            if 7 <= b + 6 < B:
                load_residual(b + 6)
            if 0 <= b - 4 < B - 2:
                add_late_bias(b - 4, natural[min(b + 2, B - 1)][3])
            if 0 <= b - 3 < B:
                add_residual(b - 3)
            if 1 <= b - 1 < B:
                add_direct_bias(b - 1)
            if 3 <= b + 3 < B:
                double_attention(b + 3)
            if 2 <= b + 1 < B:
                quantise_streams(b + 1)
            if 2 <= b + 2 < B:
                turn_streams(b + 2)
            if 1 <= b - 1 < B:
                turn_graph(b - 1)
            if 1 <= b < B:
                begin_graph(b)
            if 1 <= b < B:
                graph_turned(b, 0, 4)
            if 1 <= b < B:
                graph_direct(b)
            if 1 <= b < B:
                graph_turned(b, 4, BLOCKS)
            if 0 <= b - 2 < B:
                output_sums(b - 2)
            if 3 <= b + 3 < B:
                fuse_streams(b + 3)
            if 0 <= b - 2 < B:
                add_proj_bias(b - 2)
            if 1 <= b - 1 < B:
                quantise_graph(b - 1)
            if 0 <= b - 4 < B:
                store(b - 4)
            if b == 0:
                quantise_proj_weight()
                quantise_graph(0)
